import numpy as np
import ml_dtypes


def mxq(x, axis, fmt="e4m3"):
    dtype, down = {"e4m3": (ml_dtypes.float8_e4m3fn, 7), "e5m2": (ml_dtypes.float8_e5m2, 14)}[fmt]
    v = np.moveaxis(np.asarray(x, np.float32).astype(ml_dtypes.bfloat16).astype(np.float64), axis, -1)
    blocks = v.reshape(v.shape[:-1] + (-1, 32))
    amax = np.abs(blocks).max(-1, keepdims=True)
    byte = np.maximum(np.where(amax > 0, np.frexp(amax)[1] - 1 + 127, 0) - down, 1)
    scale = np.exp2(byte - 127.0)
    codes = (blocks / scale).astype(np.float32).astype(dtype).astype(np.float64)
    return np.moveaxis((codes * scale).reshape(v.shape), -1, axis)


WIDE = False


def mx_kscale(k):
    if not WIDE:
        return np.ones(k)
    levels = np.array([10, -10, 5, -5, 0])
    if k % 512:
        return np.exp2(np.random.permutation(np.resize(levels, k // 32))).repeat(32)
    a = np.empty((k // 512, 16))
    for p in range(k // 512):
        a[p, :8] = np.random.permutation(np.resize(levels, 8))
        for g in range(8):
            far = levels[np.abs(levels - a[p, g]) >= 10]
            a[p, g + 8] = far[np.random.randint(len(far))]
    return np.exp2(a.ravel()).repeat(32)


BF16 = ml_dtypes.bfloat16


def bf(x):
    return np.asarray(x, np.float32).astype(BF16)


def f64(x):
    return np.asarray(x).astype(np.float64)


M, B, I, H, O = 5, 2048, 128, 512, 64
O2 = 2 * O
EPS = 1e-6


def softplus(v):
    return np.maximum(v, 0.0) + np.log(1.0 + np.exp(-np.abs(v)))


def setup_inputs():
    s, t = mx_kscale(H), mx_kscale(H)
    return {"h1": bf(np.maximum(np.random.standard_normal((M, B, H)), 0.0) * s),
            "W2": bf(np.random.standard_normal((M, H, H)) * 1.4 / np.sqrt(H) * t[None, :, None] / s[None, None, :]),
            "b2": bf(np.random.standard_normal((M, H)) * 0.3 * t),
            "W3": bf(np.random.standard_normal((M, O2, H)) * 1.4 / np.sqrt(H) / t[None, None, :]),
            "b3": bf(np.random.standard_normal((M, O2)) * 0.3)}


def reference(h1, W2, b2, W3, b3):
    h2 = np.maximum((mxq(f64(h1), 2, "e4m3") @ mxq(f64(W2), 2, "e4m3").transpose(0, 2, 1)) + f64(b2)[:, None, :], 0.0)
    y = (mxq(h2, 2, "e4m3") @ mxq(f64(W3), 2, "e4m3").transpose(0, 2, 1)) + f64(b3)[:, None, :]
    means = y[:, :, :O]
    variances = softplus(y[:, :, O:]) + EPS
    mean = means.mean(axis=0)
    variance = (variances + means ** 2).mean(axis=0) - mean ** 2
    variance = np.maximum(variance, 0.0) + EPS
    return mean, variance

@@ -1,0 +1,477 @@
+import math
+from contextlib import ExitStack
+
+import concourse.mybir as mybir
+from concourse.masks import make_identity
+
+F32 = mybir.dt.float32
+BF16 = mybir.dt.bfloat16
+U32 = mybir.dt.uint32
+U8 = mybir.dt.uint8
+FP8X4 = mybir.dt.float8_e4m3fn_x4
+ALU = mybir.AluOpType
+ACT = mybir.ActivationFunctionType
+
+P = 128
+M = 5
+B = 2048
+H = 512
+O = 64
+O2 = 128
+CH = 512
+NCH = B // CH
+R = CH // P
+NU = NCH * M
+EPS = 1e-6
+CLAMP = 14.0
+DELTA = 1.0 / (1.0 + math.exp(CLAMP))
+LN_SCALE = 2.0 ** 40
+
+FLOPS = 2 * M * B * H * H + 2 * M * B * H * O2
+
+
+def tile_gaussianmixturemlp_pa_kernel(tc, h1, W2, b2, W3, b3, out_0, out_1):
+    nc = tc.nc
+    with ExitStack() as ctx:
+        const = ctx.enter_context(tc.tile_pool(name="const", bufs=1))
+        keep = ctx.enter_context(tc.tile_pool(name="keep", bufs=1))
+        wraw = ctx.enter_context(tc.tile_pool(name="wraw", bufs=2))
+        xin = ctx.enter_context(tc.tile_pool(name="xin", bufs=5))
+        work = ctx.enter_context(tc.tile_pool(name="work", bufs=3))
+        codes = ctx.enter_context(tc.tile_pool(name="codes", bufs=3))
+        epi = ctx.enter_context(tc.tile_pool(name="epi", bufs=3))
+        psum = ctx.enter_context(tc.psum_pool(name="psum", bufs=8))
+        ctx.enter_context(tc.manual_schedule())
+
+        ident = const.tile([P, P], F32)
+        neg_clamp = const.tile([P, 1], F32)
+        ones = const.tile([P, 1], F32)
+        ln_shift = const.tile([P, 1], F32)
+        table_warm = const.tile([P, 1], F32)
+        acc_init = const.tile([P, 1], F32)
+        b2raw = const.tile([P, M, 4], BF16)
+        b2f = const.tile([P, M, 4], F32)
+        b3raw = const.tile([P, M, O2], BF16)
+        b3f = const.tile([P, M, O2], F32)
+        b3m = const.tile([P, O], F32)
+        zeros = const.tile([P, CH], BF16)
+
+        w2c = keep.tile([P, M, H], U32, align_bytes=64)
+        w2s = keep.tile([P, M, H], U8, align_bytes=64)
+        w3c = keep.tile([P, M, O2], U32, align_bytes=64)
+        w3s = keep.tile([P, M, O2], U8, align_bytes=64)
+        q_all = keep.tile([P, NCH, R * O], F32)
+        a2_all = keep.tile([P, NCH, R * O], F32)
+        lnq = keep.tile([P, NCH, R * O], F32)
+        var = keep.tile([P, NCH, R * O], F32)
+
+        unit = {}
+        wt = {}
+        chunk = {}
+
+        def valid(u):
+            return 0 <= u < NU
+
+        def idle_plain(n):
+            scratch = psum.tile([P, CH], F32, tag="bank")
+            for k in range(n):
+                nc.tensor.matmul(out=scratch[:], lhsT=zeros[:, 0:P], rhs=zeros[:], start=True, stop=True)
+
+        def load_bias3():
+            nc.sync.dma_start(
+                out=b3raw[:].rearrange("p m o -> p (m o)"),
+                in_=b3.rearrange("m o -> (m o)").partition_broadcast(P),
+            )
+
+        def setup():
+            nc.vector.memset(zeros[:], 0.0)
+            idle_plain(4)
+            make_identity(nc, ident[:])
+            nc.vector.memset(neg_clamp[:], -CLAMP)
+            nc.vector.memset(ones[:], 1.0)
+            nc.scalar.dma_start(out=b2raw[:], in_=b2.rearrange("m (p t) -> p m t", t=4))
+            nc.scalar.activation(out=ln_shift[:], in_=ones[:], func=ACT.Ln, scale=LN_SCALE)
+            nc.scalar.activation(out=table_warm[:], in_=ones[:], func=ACT.Sigmoid)
+            nc.vector.tensor_scalar(
+                out=acc_init[:], in0=ln_shift[:], scalar1=0.5, scalar2=0.5 * M * EPS, op0=ALU.mult, op1=ALU.add
+            )
+
+        def bias2():
+            nc.vector.tensor_copy(out=b2f[:], in_=b2raw[:])
+
+        def bias3():
+            nc.vector.tensor_copy(out=b3f[:, :, 0:O], in_=b3raw[:, :, 0:O])
+            nc.vector.tensor_scalar_add(out=b3f[:, :, O:O2], in0=b3raw[:, :, O:O2], scalar1=-CLAMP)
+            nc.vector.tensor_reduce(
+                out=b3m[:],
+                in_=b3f[:, :, 0:O].rearrange("p m o -> p o m"),
+                axis=mybir.AxisListType.X,
+                op=ALU.add,
+            )
+            nc.vector.tensor_scalar_mul(out=b3m[:], in0=b3m[:], scalar1=1.0 / M)
+
+        def load_w(m):
+            w2raw = wraw.tile([P, 4 * H], BF16, tag="w2raw")
+            nc.sync.dma_start(out=w2raw[:], in_=W2[m].rearrange("(p t) k -> p (t k)", t=4))
+            w3raw = wraw.tile([P, H], BF16, tag="w3raw")
+            nc.sync.dma_start(out=w3raw[:], in_=W3[m])
+            wt[m] = {"w2raw": w2raw, "w3raw": w3raw}
+
+        def load_x(u):
+            if not valid(u):
+                return
+            m, c = divmod(u, NCH)
+            x = xin.tile([P, R * H], BF16, tag="x")
+            nc.sync.dma_start(
+                out=x[:], in_=h1[m, c * CH : (c + 1) * CH, :].rearrange("(p r) k -> p (r k)", r=R)
+            )
+            unit[u] = {"x": x}
+
+        def transpose_pair(src_words, j):
+            bank = psum.tile([P, 2, 2, P], F32, tag="bank")
+            for a in range(2):
+                for w in range(2):
+                    off = (2 * j + a) * 256
+                    nc.tensor.transpose(bank[:, a, w, :], src_words[:, off + w : off + 256 : 2], ident[:])
+            return bank
+
+        def words_out(copy, grouped, j, bank):
+            dst = grouped[:].bitcast(F32).rearrange("q (r c w) -> q r c w", c=P, w=2)
+            copy(out=dst[:, 2 * j : 2 * j + 2], in_=bank[:].rearrange("q a w c -> q a c w"))
+
+        def w_transposes(m, j):
+            d = wt[m]
+            if j < 2:
+                d["tp%d" % j] = transpose_pair(d["w2raw"][:].bitcast(F32), j)
+            else:
+                w3w = d["w3raw"][:].bitcast(F32).rearrange("o (p w) -> o p w", w=2)
+                bank3 = psum.tile([P, 2, 2, P], F32, tag="bank")
+                for w in range(2):
+                    nc.tensor.transpose(bank3[:, 0, w, :], w3w[:, :, w], ident[:])
+                d["tp2"] = bank3
+
+        def w_exit(m, j):
+            d = wt[m]
+            if j == 0:
+                d["gw2"] = work.tile([P, 4 * H], BF16, align_bytes=64, tag="gw2", bufs=2, name="gw2")
+            if j < 2:
+                words_out(nc.scalar.copy if j == 1 else nc.vector.tensor_copy, d["gw2"], j, d["tp%d" % j])
+            else:
+                gw3 = work.tile([P, 4 * O2], BF16, align_bytes=64, tag="gw3", bufs=2)
+                nc.vector.tensor_copy(
+                    out=gw3[:].bitcast(F32).rearrange("p (o w) -> p o w", w=2),
+                    in_=d["tp2"][:, 0].rearrange("p w o -> p o w"),
+                )
+                d["gw3"] = gw3
+
+        def w_quantise(m):
+            d = wt[m]
+            nc.vector.quantize_mx(out=w2c[:, m, :].bitcast(FP8X4), scales=w2s[:, m, :], in_=d["gw2"][:])
+            nc.vector.quantize_mx(out=w3c[:, m, :].bitcast(FP8X4), scales=w3s[:, m, :], in_=d["gw3"][:])
+
+        def x_transposes(u, j):
+            if valid(u):
+                unit[u]["tp%d" % j] = transpose_pair(unit[u]["x"][:].bitcast(F32), j)
+
+        def x_exit(u, j):
+            if not valid(u):
+                return
+            d = unit[u]
+            if j == 0:
+                d["g1"] = work.tile([P, 4 * CH], BF16, align_bytes=64, tag="g1", name="g1")
+            words_out(nc.scalar.copy, d["g1"], j, d["tp%d" % j])
+
+        def quantise1(u):
+            if not valid(u):
+                return
+            d = unit[u]
+            c1 = codes.tile([P, CH], U32, align_bytes=64, tag="c1")
+            s1 = codes.tile([P, CH], U8, align_bytes=64, tag="s1")
+            nc.vector.quantize_mx(out=c1[:].bitcast(FP8X4), scales=s1[:], in_=d["g1"][:])
+            d["c1"] = c1
+            d["s1"] = s1
+
+        def layer1(u, t):
+            if not valid(u):
+                return
+            d = unit[u]
+            m = u // NCH
+            acc1 = psum.tile([P, CH], F32, tag="bank")
+            nc.tensor.matmul_mx(
+                out=acc1[:],
+                lhsT=w2c[:, m, t * P : (t + 1) * P].bitcast(FP8X4),
+                lhsT_scale=w2s[:, m, t * P : (t + 1) * P],
+                rhs=d["c1"][:].bitcast(FP8X4),
+                rhs_scale=d["s1"][:],
+                start=True,
+                stop=True,
+            )
+            d["l1_%d" % t] = acc1
+
+        def h2_exit(u, t):
+            if not valid(u):
+                return
+            d = unit[u]
+            m = u // NCH
+            if t == 0:
+                d["planes"] = work.tile([P, 4, CH], BF16, tag="planes", name="planes")
+            nc.scalar.activation(
+                out=d["planes"][:, t, :],
+                in_=d["l1_%d" % t][:],
+                func=ACT.Relu,
+                bias=b2f[:, m, t : t + 1],
+                scale=1.0,
+            )
+
+        def regroup(u):
+            if not valid(u):
+                return
+            d = unit[u]
+            g2 = work.tile([P, 4 * CH], BF16, align_bytes=64, tag="g2")
+            nc.vector.tensor_copy(
+                out=g2[:].rearrange("p (c i t) -> p c t i", i=4, t=4),
+                in_=d["planes"][:].rearrange("p t (c i) -> p c t i", i=4),
+            )
+            d["g2"] = g2
+
+        def quantise2(u):
+            if not valid(u):
+                return
+            d = unit[u]
+            c2 = codes.tile([P, CH], U32, align_bytes=64, tag="c2", bufs=NU)
+            s2 = codes.tile([P, CH], U8, align_bytes=64, tag="s2", bufs=NU)
+            nc.vector.quantize_mx(out=c2[:].bitcast(FP8X4), scales=s2[:], in_=d["g2"][:])
+            d["c2"] = c2
+            d["s2"] = s2
+
+        def layer2_pass(out, u, r, start, stop):
+            d = unit[u]
+            m = u // NCH
+            nc.tensor.matmul_mx(
+                out=out,
+                lhsT=d["c2"][:, r * P : (r + 1) * P].bitcast(FP8X4),
+                lhsT_scale=d["s2"][:, r * P : (r + 1) * P],
+                rhs=w3c[:, m, :].bitcast(FP8X4),
+                rhs_scale=w3s[:, m, :],
+                start=start,
+                stop=stop,
+            )
+
+        def hold_clock(u, n):
+            if not valid(u):
+                return
+            yb = psum.tile([P, R, O2], F32, tag="bank")
+            for k in range(n):
+                nc.tensor.matmul_mx(
+                    out=yb[:].rearrange("p r o -> p (r o)"),
+                    lhsT=w2c[:, 0, 0:P].bitcast(FP8X4),
+                    lhsT_scale=w2s[:, 0, 0:P],
+                    rhs=w2c[:, 0, :].bitcast(FP8X4),
+                    rhs_scale=w2s[:, 0, :],
+                    start=True,
+                    stop=True,
+                )
+            unit[u]["yb"] = yb
+
+        def layer2(u):
+            if not valid(u):
+                return
+            yb = unit[u]["yb"]
+            for r in range(R):
+                layer2_pass(yb[:, r, :], u, r, True, True)
+            if u // NCH == M - 1:
+                c = u % NCH
+                tb = psum.tile([P, R, O2], F32, tag="bank")
+                for r in range(R):
+                    for m in range(M):
+                        layer2_pass(tb[:, r, :], m * NCH + c, r, m == 0, m == M - 1)
+                chunk[c]["tb"] = tb
+
+        def add_bias3(u):
+            if not valid(u):
+                return
+            d = unit[u]
+            m = u // NCH
+            y = epi.tile([P, R, O2], F32, tag="y")
+            nc.vector.tensor_tensor(
+                out=y[:],
+                in0=d["yb"][:],
+                in1=b3f[:, m, :].unsqueeze(1).to_broadcast([P, R, O2]),
+                op=ALU.add,
+            )
+            d["y"] = y
+
+        def nonlinear(u):
+            if not valid(u):
+                return
+            d = unit[u]
+            y = d["y"]
+            sg = epi.tile([P, R, O], F32, tag="sg")
+            nc.scalar.activation(
+                out=sg[:], in_=y[:, :, O:O2], func=ACT.Sigmoid, bias=neg_clamp[:], scale=-1.0
+            )
+            nc.scalar.activation(out=y[:, :, 0:O], in_=y[:, :, 0:O], func=ACT.Square)
+            d["sg"] = sg
+
+        def accumulate(u):
+            if not valid(u):
+                return
+            d = unit[u]
+            m, c = divmod(u, NCH)
+            if m == 0:
+                chunk[c] = {"acc": epi.tile([P, R, O2], F32, tag="acc", bufs=NCH, name="acc")}
+            q = q_all[:, c, :]
+            sgf = d["sg"][:].rearrange("p r o -> p (r o)")
+            yf = d["y"][:].rearrange("p r o -> p (r o)")
+            accf = chunk[c]["acc"][:].rearrange("p r o -> p (r o)")
+            if m == 0:
+                nc.vector.tensor_scalar_max(out=q, in0=sgf, scalar1=DELTA)
+                nc.vector.tensor_scalar(
+                    out=accf, in0=yf, scalar1=0.0, scalar2=acc_init[:, 0:1], op0=ALU.max, op1=ALU.add
+                )
+            else:
+                nc.vector.scalar_tensor_tensor(out=q, in0=sgf, scalar=DELTA, in1=q, op0=ALU.max, op1=ALU.mult)
+                nc.vector.scalar_tensor_tensor(out=accf, in0=yf, scalar=0.0, in1=accf, op0=ALU.max, op1=ALU.add)
+
+        def mean_of(c):
+            d = chunk[c]
+            mean = epi.tile([P, R, O], F32, tag="mean", bufs=2)
+            nc.vector.scalar_tensor_tensor(
+                out=mean[:],
+                in0=d["tb"][:, :, 0:O],
+                scalar=1.0 / M,
+                in1=b3m[:].unsqueeze(1).to_broadcast([P, R, O]),
+                op0=ALU.mult,
+                op1=ALU.add,
+            )
+            nc.sync.dma_start(
+                out=out_0[c * CH : (c + 1) * CH, :].rearrange("(p r) o -> p (r o)", r=R),
+                in_=mean[:].rearrange("p r o -> p (r o)"),
+            )
+            d["mean"] = mean
+
+        def mean_square(c):
+            d = chunk[c]
+            msq = epi.tile([P, R, O], F32, tag="msq", bufs=2)
+            nc.scalar.activation(out=msq[:], in_=d["mean"][:], func=ACT.Square)
+            d["msq"] = msq
+
+        def spread_sum(c):
+            d = chunk[c]
+            a1 = epi.tile([P, R, O], F32, tag="a1", bufs=2)
+            nc.vector.tensor_tensor(out=a1[:], in0=d["acc"][:, :, 0:O], in1=d["acc"][:, :, O:O2], op=ALU.add)
+            d["a1"] = a1
+
+        def spread_of(c):
+            d = chunk[c]
+            nc.vector.scalar_tensor_tensor(
+                out=a2_all[:, c, :],
+                in0=d["a1"][:].rearrange("p r o -> p (r o)"),
+                scalar=1.0 / M,
+                in1=d["msq"][:].rearrange("p r o -> p (r o)"),
+                op0=ALU.mult,
+                op1=ALU.subtract,
+            )
+
+        def log_of(c0, c1):
+            nc.scalar.activation(out=lnq[:, c0:c1, :], in_=q_all[:, c0:c1, :], func=ACT.Ln, scale=LN_SCALE)
+
+        def variance_of(c0, c1):
+            v = var[:, c0:c1, :].rearrange("p c f -> p (c f)")
+            nc.vector.scalar_tensor_tensor(
+                out=v,
+                in0=lnq[:, c0:c1, :].rearrange("p c f -> p (c f)"),
+                scalar=-1.0 / M,
+                in1=a2_all[:, c0:c1, :].rearrange("p c f -> p (c f)"),
+                op0=ALU.mult,
+                op1=ALU.add,
+            )
+            nc.vector.tensor_scalar(out=v, in0=v, scalar1=0.0, scalar2=EPS, op0=ALU.max, op1=ALU.add)
+            for c in range(c0, c1):
+                nc.sync.dma_start(
+                    out=out_1[c * CH : (c + 1) * CH, :].rearrange("(p r) o -> p (r o)", r=R), in_=var[:, c, :]
+                )
+
+        load_w(0)
+        load_x(0)
+        setup()
+        load_x(1)
+        load_x(2)
+        for i in range(-2, NU):
+            if i >= -1:
+                load_x(i + 4)
+            if i == 0:
+                load_bias3()
+            if i == -2:
+                load_w(1)
+            elif i % NCH == 1 and i // NCH + 2 < M:
+                load_w(i // NCH + 2)
+            piece = (i // NCH + 1, i % NCH) if (i >= 0 and i % NCH < 3 and i // NCH + 1 < M) else None
+            done = (i - 2) % NCH if (valid(i - 2) and (i - 2) // NCH == M - 1) else -1
+            add_bias3(i - 2)
+            x_exit(i + 1, 0)
+            x_exit(i + 1, 1)
+            if i == -2:
+                for j in range(3):
+                    w_transposes(0, j)
+                    w_exit(0, j)
+            x_transposes(i + 2, 0)
+            x_transposes(i + 2, 1)
+            if piece:
+                w_transposes(piece[0], piece[1])
+            if i < 1:
+                idle_plain(1)
+            hold_clock(i - 1, 2)
+            regroup(i - 1)
+            quantise1(i + 1)
+            if done >= 0:
+                mean_of(done)
+            h2_exit(i, 0)
+            if piece:
+                w_exit(piece[0], piece[1])
+                if piece[1] == 2:
+                    w_quantise(piece[0])
+            if i == -2:
+                w_quantise(0)
+                bias2()
+            if i == 1:
+                bias3()
+            nonlinear(i - 2)
+            if done >= 0:
+                mean_square(done)
+            layer1(i + 1, 0)
+            h2_exit(i, 1)
+            layer1(i + 1, 1)
+            quantise2(i - 1)
+            layer2(i - 1)
+            accumulate(i - 2)
+            if done >= 0:
+                spread_sum(done)
+                spread_of(done)
+            h2_exit(i, 2)
+            layer1(i + 1, 2)
+            h2_exit(i, 3)
+            layer1(i + 1, 3)
+        last = NU - 1
+        hold_clock(last, 3)
+        regroup(last)
+        quantise2(last)
+        add_bias3(last - 1)
+        mean_of(NCH - 2)
+        layer2(last)
+        nonlinear(last - 1)
+        mean_square(NCH - 2)
+        add_bias3(last)
+        nonlinear(last)
+        accumulate(last - 1)
+        log_of(0, NCH - 2)
+        spread_sum(NCH - 2)
+        spread_of(NCH - 2)
+        accumulate(last)
+        mean_of(NCH - 1)
+        spread_sum(NCH - 1)
+        mean_square(NCH - 1)
+        log_of(NCH - 2, NCH)
+        variance_of(0, NCH - 2)
+        spread_of(NCH - 1)
+        variance_of(NCH - 2, NCH)

@@ -19,9 +19,11 @@ H = 512
 O = 64
 O2 = 128
 CH = 512
-NCH = B // CH
 R = CH // P
-NU = NCH * M
+NP = B // (2 * CH)
+NU = NP * M * 2
+NK = NP * M
+WP = 320
 EPS = 1e-6
 CLAMP = 14.0
 DELTA = 1.0 / (1.0 + math.exp(CLAMP))
@@ -39,92 +41,122 @@ def tile_gaussianmixturemlp_pa_kernel(tc, h1, W2, b2, W3, b3, out_0, out_1):
         xin = ctx.enter_context(tc.tile_pool(name="xin", bufs=5))
         work = ctx.enter_context(tc.tile_pool(name="work", bufs=3))
         codes = ctx.enter_context(tc.tile_pool(name="codes", bufs=3))
-        epi = ctx.enter_context(tc.tile_pool(name="epi", bufs=3))
-        psum = ctx.enter_context(tc.psum_pool(name="psum", bufs=8))
+        epi = ctx.enter_context(tc.tile_pool(name="epi", bufs=2))
+        psum = ctx.enter_context(tc.psum_pool(name="psum", bufs=6))
         ctx.enter_context(tc.manual_schedule())
 
         ident = const.tile([P, P], F32)
-        neg_clamp = const.tile([P, 1], F32)
+        identb = const.tile([P, 8], BF16)
         ones = const.tile([P, 1], F32)
-        ln_shift = const.tile([P, 1], F32)
         table_warm = const.tile([P, 1], F32)
-        acc_init = const.tile([P, 1], F32)
         b2raw = const.tile([P, M, 4], BF16)
         b2f = const.tile([P, M, 4], F32)
-        b3raw = const.tile([P, M, O2], BF16)
-        b3f = const.tile([P, M, O2], F32)
-        b3m = const.tile([P, O], F32)
+        b3rows = const.tile([P, 2, O], BF16)
+        b3twice = const.tile([P, 2, 2, O], BF16)
+        b3cols = const.tile([P, 2, 8], F32)
+        neg_raw = const.tile([P, M], F32)
+        edge = const.tile([P, M], F32)
+        mean_bias = const.tile([P, 1], F32)
+        shift = const.tile([P, 1], F32)
         zeros = const.tile([P, CH], BF16)
 
         w2c = keep.tile([P, M, H], U32, align_bytes=64)
         w2s = keep.tile([P, M, H], U8, align_bytes=64)
-        w3c = keep.tile([P, M, O2], U32, align_bytes=64)
-        w3s = keep.tile([P, M, O2], U8, align_bytes=64)
-        q_all = keep.tile([P, NCH, R * O], F32)
-        a2_all = keep.tile([P, NCH, R * O], F32)
-        lnq = keep.tile([P, NCH, R * O], F32)
-        var = keep.tile([P, NCH, R * O], F32)
+        w3c = keep.tile([P, M, WP], U32, align_bytes=64)
+        w3s = keep.tile([P, M, WP], U8, align_bytes=64)
+        q = keep.tile([P, NP, CH], F32)
+        acc = keep.tile([P, NP, CH], F32)
+        lnq = keep.tile([P, NP, CH], F32)
+        spread = keep.tile([P, NP, CH], F32)
+        msq = keep.tile([P, NP, CH], F32)
+        mean_p = keep.tile([P, NP, CH], F32)
+        var_p = keep.tile([P, NP, CH], F32)
 
         unit = {}
         wt = {}
-        chunk = {}
+        pair = {k: {} for k in range(NK)}
+        group = {}
 
         def valid(u):
             return 0 <= u < NU
 
+        def place(u):
+            k, h = divmod(u, 2)
+            pr, m = divmod(k, M)
+            return pr, m, h
+
         def idle_plain(n):
-            scratch = psum.tile([P, CH], F32, tag="bank")
-            for k in range(n):
+            scratch = psum.tile([P, CH], F32, tag="head", bufs=1, name="scratch")
+            for j in range(n):
                 nc.tensor.matmul(out=scratch[:], lhsT=zeros[:, 0:P], rhs=zeros[:], start=True, stop=True)
 
-        def load_bias3():
-            nc.sync.dma_start(
-                out=b3raw[:].rearrange("p m o -> p (m o)"),
-                in_=b3.rearrange("m o -> (m o)").partition_broadcast(P),
-            )
-
         def setup():
+            nc.vector.memset(b3rows[:].rearrange("p s o -> p (s o)"), 0.0)
+            nc.scalar.dma_start(out=b3rows[0:M].rearrange("m s o -> m (s o)"), in_=b3)
+            nc.scalar.dma_start(out=b2raw[:], in_=b2.rearrange("m (p t) -> p m t", t=4))
             nc.vector.memset(zeros[:], 0.0)
             idle_plain(4)
             make_identity(nc, ident[:])
-            nc.vector.memset(neg_clamp[:], -CLAMP)
             nc.vector.memset(ones[:], 1.0)
-            nc.scalar.dma_start(out=b2raw[:], in_=b2.rearrange("m (p t) -> p m t", t=4))
-            nc.scalar.activation(out=ln_shift[:], in_=ones[:], func=ACT.Ln, scale=LN_SCALE)
+            nc.vector.memset(w3c[:], 0)
+            nc.vector.memset(w3s[:].rearrange("p m w -> p (m w)").bitcast(U32), 0)
             nc.scalar.activation(out=table_warm[:], in_=ones[:], func=ACT.Sigmoid)
-            nc.vector.tensor_scalar(
-                out=acc_init[:], in0=ln_shift[:], scalar1=0.5, scalar2=0.5 * M * EPS, op0=ALU.mult, op1=ALU.add
-            )
 
         def bias2():
             nc.vector.tensor_copy(out=b2f[:], in_=b2raw[:])
 
-        def bias3():
-            nc.vector.tensor_copy(out=b3f[:, :, 0:O], in_=b3raw[:, :, 0:O])
-            nc.vector.tensor_scalar_add(out=b3f[:, :, O:O2], in0=b3raw[:, :, O:O2], scalar1=-CLAMP)
-            nc.vector.tensor_reduce(
-                out=b3m[:],
-                in_=b3f[:, :, 0:O].rearrange("p m o -> p o m"),
-                axis=mybir.AxisListType.X,
-                op=ALU.add,
-            )
-            nc.vector.tensor_scalar_mul(out=b3m[:], in0=b3m[:], scalar1=1.0 / M)
+        def bias3_twice():
+            nc.vector.tensor_copy(out=identb[:], in_=ident[:, 0:8])
+            nc.vector.tensor_copy(out=b3twice[:], in_=b3rows[:].unsqueeze(2).to_broadcast([P, 2, 2, O]))
 
-        def load_w(m):
+        def bias3_turn():
+            turned = psum.tile([P, 2, 8], F32, tag="head", bufs=1, name="turned")
+            for s in range(2):
+                nc.tensor.matmul(
+                    out=turned[:, s, :], lhsT=b3twice[:, s].rearrange("p d o -> p (d o)"), rhs=identb[:],
+                    start=True, stop=True,
+                )
+            group["turned"] = turned
+
+        def bias3():
+            nc.vector.tensor_copy(out=b3cols[:], in_=group["turned"][:])
+            nc.vector.tensor_scalar_mul(out=neg_raw[:], in0=b3cols[:, 1, 0:M], scalar1=-1.0)
+            nc.vector.tensor_reduce(out=mean_bias[:], in_=b3cols[:, 0, 0:M], axis=mybir.AxisListType.X, op=ALU.add)
+            nc.vector.tensor_scalar_add(out=edge[:], in0=neg_raw[:], scalar1=CLAMP)
+            nc.vector.tensor_scalar_mul(out=mean_bias[:], in0=mean_bias[:], scalar1=1.0 / M)
+            nc.vector.tensor_reduce(out=shift[:], in_=edge[:], axis=mybir.AxisListType.X, op=ALU.add)
+            nc.vector.tensor_scalar(
+                out=shift[:], in0=shift[:], scalar1=-1.0 / M, scalar2=math.log(LN_SCALE) / M + 2 * EPS,
+                op0=ALU.mult, op1=ALU.add,
+            )
+
+        def load_w2(m, pieces=1):
             w2raw = wraw.tile([P, 4 * H], BF16, tag="w2raw")
-            nc.sync.dma_start(out=w2raw[:], in_=W2[m].rearrange("(p t) k -> p (t k)", t=4))
+            n = 4 * H // pieces
+            for j in range(pieces):
+                nc.sync.dma_start(
+                    out=w2raw[:, j * n : (j + 1) * n],
+                    in_=W2[m].rearrange("(p t) k -> p (t k)", t=4)[:, j * n : (j + 1) * n],
+                )
+            wt.setdefault(m, {})["w2raw"] = w2raw
+
+        def load_w3(m):
             w3raw = wraw.tile([P, H], BF16, tag="w3raw")
             nc.sync.dma_start(out=w3raw[:], in_=W3[m])
-            wt[m] = {"w2raw": w2raw, "w3raw": w3raw}
+            wt.setdefault(m, {})["w3raw"] = w3raw
 
-        def load_x(u):
+        def load_x(u, pieces=1):
             if not valid(u):
                 return
-            m, c = divmod(u, NCH)
+            pr, m, h = place(u)
+            c = 2 * pr + h
             x = xin.tile([P, R * H], BF16, tag="x")
-            nc.sync.dma_start(
-                out=x[:], in_=h1[m, c * CH : (c + 1) * CH, :].rearrange("(p r) k -> p (r k)", r=R)
-            )
+            n = R * H // pieces
+            for j in range(pieces):
+                nc.sync.dma_start(
+                    out=x[:, j * n : (j + 1) * n],
+                    in_=h1[m, c * CH : (c + 1) * CH, :].rearrange("(p r) k -> p (r k)", r=R)[:, j * n : (j + 1) * n],
+                )
             unit[u] = {"x": x}
 
         def transpose_pair(src_words, j):
@@ -139,47 +171,57 @@ def tile_gaussianmixturemlp_pa_kernel(tc, h1, W2, b2, W3, b3, out_0, out_1):
             dst = grouped[:].bitcast(F32).rearrange("q (r c w) -> q r c w", c=P, w=2)
             copy(out=dst[:, 2 * j : 2 * j + 2], in_=bank[:].rearrange("q a w c -> q a c w"))
 
-        def w_transposes(m, j):
+        def w2_transposes(m, j):
             d = wt[m]
-            if j < 2:
-                d["tp%d" % j] = transpose_pair(d["w2raw"][:].bitcast(F32), j)
-            else:
-                w3w = d["w3raw"][:].bitcast(F32).rearrange("o (p w) -> o p w", w=2)
-                bank3 = psum.tile([P, 2, 2, P], F32, tag="bank")
-                for w in range(2):
-                    nc.tensor.transpose(bank3[:, 0, w, :], w3w[:, :, w], ident[:])
-                d["tp2"] = bank3
+            d["tp%d" % j] = transpose_pair(d["w2raw"][:].bitcast(F32), j)
 
-        def w_exit(m, j):
+        def w2_exit(m, j, copy):
             d = wt[m]
             if j == 0:
                 d["gw2"] = work.tile([P, 4 * H], BF16, align_bytes=64, tag="gw2", bufs=2, name="gw2")
-            if j < 2:
-                words_out(nc.scalar.copy if j == 1 else nc.vector.tensor_copy, d["gw2"], j, d["tp%d" % j])
-            else:
-                gw3 = work.tile([P, 4 * O2], BF16, align_bytes=64, tag="gw3", bufs=2)
-                nc.vector.tensor_copy(
-                    out=gw3[:].bitcast(F32).rearrange("p (o w) -> p o w", w=2),
-                    in_=d["tp2"][:, 0].rearrange("p w o -> p o w"),
-                )
-                d["gw3"] = gw3
+            words_out(copy, d["gw2"], j, d["tp%d" % j])
 
-        def w_quantise(m):
+        def w2_quantise(m):
+            nc.vector.quantize_mx(out=w2c[:, m, :].bitcast(FP8X4), scales=w2s[:, m, :], in_=wt[m]["gw2"][:])
+
+        def w3_transposes(m):
             d = wt[m]
-            nc.vector.quantize_mx(out=w2c[:, m, :].bitcast(FP8X4), scales=w2s[:, m, :], in_=d["gw2"][:])
-            nc.vector.quantize_mx(out=w3c[:, m, :].bitcast(FP8X4), scales=w3s[:, m, :], in_=d["gw3"][:])
+            w3w = d["w3raw"][:].bitcast(F32).rearrange("o (p w) -> o p w", w=2)
+            bank = psum.tile([P, 2, P], F32, tag="bank")
+            for w in range(2):
+                nc.tensor.transpose(bank[:, w, :], w3w[:, :, w], ident[:])
+            d["tp2"] = bank
 
-        def x_transposes(u, j):
+        def w3_exit(m):
+            d = wt[m]
+            gw3 = work.tile([P, 4 * O2], BF16, align_bytes=64, tag="gw3", bufs=2)
+            nc.vector.tensor_copy(
+                out=gw3[:].bitcast(F32).rearrange("p (o w) -> p o w", w=2),
+                in_=d["tp2"][:].rearrange("p w o -> p o w"),
+            )
+            d["gw3"] = gw3
+
+        def w3_quantise(m):
+            for s in range(2):
+                cols = slice((2 * s + 1) * O, (2 * s + 2) * O)
+                nc.vector.quantize_mx(
+                    out=w3c[:, m, cols].bitcast(FP8X4),
+                    scales=w3s[:, m, cols],
+                    in_=wt[m]["gw3"][:, s * 4 * O : (s + 1) * 4 * O],
+                )
+
+        def x_transposes(u):
             if valid(u):
-                unit[u]["tp%d" % j] = transpose_pair(unit[u]["x"][:].bitcast(F32), j)
+                for j in range(2):
+                    unit[u]["tp%d" % j] = transpose_pair(unit[u]["x"][:].bitcast(F32), j)
 
-        def x_exit(u, j):
+        def x_exit(u, j, copy):
             if not valid(u):
                 return
             d = unit[u]
             if j == 0:
                 d["g1"] = work.tile([P, 4 * CH], BF16, align_bytes=64, tag="g1", name="g1")
-            words_out(nc.scalar.copy, d["g1"], j, d["tp%d" % j])
+            words_out(copy, d["g1"], j, d["tp%d" % j])
 
         def quantise1(u):
             if not valid(u):
@@ -195,7 +237,7 @@ def tile_gaussianmixturemlp_pa_kernel(tc, h1, W2, b2, W3, b3, out_0, out_1):
             if not valid(u):
                 return
             d = unit[u]
-            m = u // NCH
+            m = place(u)[1]
             acc1 = psum.tile([P, CH], F32, tag="bank")
             nc.tensor.matmul_mx(
                 out=acc1[:],
@@ -208,20 +250,22 @@ def tile_gaussianmixturemlp_pa_kernel(tc, h1, W2, b2, W3, b3, out_0, out_1):
             )
             d["l1_%d" % t] = acc1
 
-        def h2_exit(u, t):
+        def h2_exit(u, t, on_vector=False):
             if not valid(u):
                 return
             d = unit[u]
-            m = u // NCH
-            if t == 0:
-                d["planes"] = work.tile([P, 4, CH], BF16, tag="planes", name="planes")
-            nc.scalar.activation(
-                out=d["planes"][:, t, :],
-                in_=d["l1_%d" % t][:],
-                func=ACT.Relu,
-                bias=b2f[:, m, t : t + 1],
-                scale=1.0,
-            )
+            m = place(u)[1]
+            if "planes" not in d:
+                d["planes"] = work.tile([P, 4, CH], BF16, align_bytes=64, tag="planes", name="planes")
+            if on_vector:
+                nc.vector.tensor_scalar(
+                    out=d["planes"][:, t, :], in0=d["l1_%d" % t][:], scalar1=b2f[:, m, t : t + 1], scalar2=0.0,
+                    op0=ALU.add, op1=ALU.max,
+                )
+            else:
+                nc.scalar.activation(
+                    out=d["planes"][:, t, :], in_=d["l1_%d" % t][:], func=ACT.Relu, bias=b2f[:, m, t : t + 1], scale=1.0
+                )
 
         def regroup(u):
             if not valid(u):
@@ -238,240 +282,246 @@ def tile_gaussianmixturemlp_pa_kernel(tc, h1, W2, b2, W3, b3, out_0, out_1):
             if not valid(u):
                 return
             d = unit[u]
-            c2 = codes.tile([P, CH], U32, align_bytes=64, tag="c2", bufs=NU)
-            s2 = codes.tile([P, CH], U8, align_bytes=64, tag="s2", bufs=NU)
+            c2 = codes.tile([P, CH], U32, align_bytes=64, tag="c2", bufs=6)
+            s2 = codes.tile([P, CH], U8, align_bytes=64, tag="s2", bufs=6)
             nc.vector.quantize_mx(out=c2[:].bitcast(FP8X4), scales=s2[:], in_=d["g2"][:])
             d["c2"] = c2
             d["s2"] = s2
 
-        def layer2_pass(out, u, r, start, stop):
+        def layer2(out, u, side, start, stop):
             d = unit[u]
-            m = u // NCH
+            pr, m, h = place(u)
+            first = 2 * side * O + (1 - h) * O
             nc.tensor.matmul_mx(
                 out=out,
-                lhsT=d["c2"][:, r * P : (r + 1) * P].bitcast(FP8X4),
-                lhsT_scale=d["s2"][:, r * P : (r + 1) * P],
-                rhs=w3c[:, m, :].bitcast(FP8X4),
-                rhs_scale=w3s[:, m, :],
+                lhsT=w3c[:, m, first : first + P].bitcast(FP8X4),
+                lhsT_scale=w3s[:, m, first : first + P],
+                rhs=d["c2"][:].bitcast(FP8X4),
+                rhs_scale=d["s2"][:],
                 start=start,
                 stop=stop,
             )
 
-        def hold_clock(u, n):
-            if not valid(u):
-                return
-            yb = psum.tile([P, R, O2], F32, tag="bank")
-            for k in range(n):
-                nc.tensor.matmul_mx(
-                    out=yb[:].rearrange("p r o -> p (r o)"),
-                    lhsT=w2c[:, 0, 0:P].bitcast(FP8X4),
-                    lhsT_scale=w2s[:, 0, 0:P],
-                    rhs=w2c[:, 0, :].bitcast(FP8X4),
-                    rhs_scale=w2s[:, 0, :],
-                    start=True,
-                    stop=True,
-                )
-            unit[u]["yb"] = yb
+        def head_bank(k, side, tag, bufs):
+            pair[k][side] = psum.tile([P, CH], F32, tag=tag, bufs=bufs, name="head_bank")
 
-        def layer2(u):
-            if not valid(u):
-                return
-            yb = unit[u]["yb"]
-            for r in range(R):
-                layer2_pass(yb[:, r, :], u, r, True, True)
-            if u // NCH == M - 1:
-                c = u % NCH
-                tb = psum.tile([P, R, O2], F32, tag="bank")
-                for r in range(R):
-                    for m in range(M):
-                        layer2_pass(tb[:, r, :], m * NCH + c, r, m == 0, m == M - 1)
-                chunk[c]["tb"] = tb
+        def head_pass(k, side, h):
+            layer2(pair[k][side][:], 2 * k + h, side, h == 0, h == 1)
 
-        def add_bias3(u):
-            if not valid(u):
+        def head_passes(k, side):
+            if 0 <= k < NK:
+                head_bank(k, side, "head", 1)
+                for h in range(2):
+                    head_pass(k, side, h)
+
+        def mean_pass(k, h):
+            if not 0 <= k < NK:
                 return
-            d = unit[u]
-            m = u // NCH
-            y = epi.tile([P, R, O2], F32, tag="y")
-            nc.vector.tensor_tensor(
-                out=y[:],
-                in0=d["yb"][:],
-                in1=b3f[:, m, :].unsqueeze(1).to_broadcast([P, R, O2]),
-                op=ALU.add,
+            pr, m = divmod(k, M)
+            if m == 0 and h == 0:
+                group[pr] = psum.tile([P, CH], F32, tag="mean", bufs=1, name="mean_sum")
+            layer2(group[pr][:], 2 * k + h, 0, m == 0 and h == 0, m == M - 1 and h == 1)
+
+        def square_means(k):
+            if not 0 <= k < NK:
+                return
+            m = k % M
+            sq = epi.tile([P, CH], F32, tag="sq")
+            nc.scalar.activation(out=sq[:], in_=pair[k][0][:], func=ACT.Square, bias=b3cols[:, 0, m : m + 1], scale=1.0)
+            pair[k]["sq"] = sq
+
+        def add_squares(k):
+            if not 0 <= k < NK:
+                return
+            pr, m = divmod(k, M)
+            if m > 0:
+                nc.vector.tensor_tensor(out=acc[:, pr, :], in0=pair[k]["sq"][:], in1=acc[:, pr, :], op=ALU.add)
+
+        def sigmoid_raw(k):
+            if not 0 <= k < NK:
+                return
+            m = k % M
+            sg = epi.tile([P, CH], F32, tag="sg")
+            nc.scalar.activation(out=sg[:], in_=pair[k][1][:], func=ACT.Sigmoid, bias=neg_raw[:, m : m + 1], scale=-1.0)
+            pair[k]["sg"] = sg
+
+        def add_excess(k):
+            if not 0 <= k < NK:
+                return
+            pr, m = divmod(k, M)
+            other = pair[k]["sq"][:] if m == 0 else acc[:, pr, :]
+            nc.vector.scalar_tensor_tensor(
+                out=acc[:, pr, :], in0=pair[k][1][:], scalar=edge[:, m : m + 1], in1=other, op0=ALU.max, op1=ALU.add
             )
-            d["y"] = y
 
-        def nonlinear(u):
-            if not valid(u):
+        def multiply_sigmoid(k):
+            if not 0 <= k < NK:
                 return
-            d = unit[u]
-            y = d["y"]
-            sg = epi.tile([P, R, O], F32, tag="sg")
-            nc.scalar.activation(
-                out=sg[:], in_=y[:, :, O:O2], func=ACT.Sigmoid, bias=neg_clamp[:], scale=-1.0
-            )
-            nc.scalar.activation(out=y[:, :, 0:O], in_=y[:, :, 0:O], func=ACT.Square)
-            d["sg"] = sg
-
-        def accumulate(u):
-            if not valid(u):
-                return
-            d = unit[u]
-            m, c = divmod(u, NCH)
+            pr, m = divmod(k, M)
             if m == 0:
-                chunk[c] = {"acc": epi.tile([P, R, O2], F32, tag="acc", bufs=NCH, name="acc")}
-            q = q_all[:, c, :]
-            sgf = d["sg"][:].rearrange("p r o -> p (r o)")
-            yf = d["y"][:].rearrange("p r o -> p (r o)")
-            accf = chunk[c]["acc"][:].rearrange("p r o -> p (r o)")
-            if m == 0:
-                nc.vector.tensor_scalar_max(out=q, in0=sgf, scalar1=DELTA)
-                nc.vector.tensor_scalar(
-                    out=accf, in0=yf, scalar1=0.0, scalar2=acc_init[:, 0:1], op0=ALU.max, op1=ALU.add
-                )
+                nc.vector.tensor_scalar_max(out=q[:, pr, :], in0=pair[k]["sg"][:], scalar1=DELTA)
             else:
-                nc.vector.scalar_tensor_tensor(out=q, in0=sgf, scalar=DELTA, in1=q, op0=ALU.max, op1=ALU.mult)
-                nc.vector.scalar_tensor_tensor(out=accf, in0=yf, scalar=0.0, in1=accf, op0=ALU.max, op1=ALU.add)
-
-        def mean_of(c):
-            d = chunk[c]
-            mean = epi.tile([P, R, O], F32, tag="mean", bufs=2)
-            nc.vector.scalar_tensor_tensor(
-                out=mean[:],
-                in0=d["tb"][:, :, 0:O],
-                scalar=1.0 / M,
-                in1=b3m[:].unsqueeze(1).to_broadcast([P, R, O]),
-                op0=ALU.mult,
-                op1=ALU.add,
-            )
-            nc.sync.dma_start(
-                out=out_0[c * CH : (c + 1) * CH, :].rearrange("(p r) o -> p (r o)", r=R),
-                in_=mean[:].rearrange("p r o -> p (r o)"),
-            )
-            d["mean"] = mean
-
-        def mean_square(c):
-            d = chunk[c]
-            msq = epi.tile([P, R, O], F32, tag="msq", bufs=2)
-            nc.scalar.activation(out=msq[:], in_=d["mean"][:], func=ACT.Square)
-            d["msq"] = msq
-
-        def spread_sum(c):
-            d = chunk[c]
-            a1 = epi.tile([P, R, O], F32, tag="a1", bufs=2)
-            nc.vector.tensor_tensor(out=a1[:], in0=d["acc"][:, :, 0:O], in1=d["acc"][:, :, O:O2], op=ALU.add)
-            d["a1"] = a1
-
-        def spread_of(c):
-            d = chunk[c]
-            nc.vector.scalar_tensor_tensor(
-                out=a2_all[:, c, :],
-                in0=d["a1"][:].rearrange("p r o -> p (r o)"),
-                scalar=1.0 / M,
-                in1=d["msq"][:].rearrange("p r o -> p (r o)"),
-                op0=ALU.mult,
-                op1=ALU.subtract,
-            )
-
-        def log_of(c0, c1):
-            nc.scalar.activation(out=lnq[:, c0:c1, :], in_=q_all[:, c0:c1, :], func=ACT.Ln, scale=LN_SCALE)
-
-        def variance_of(c0, c1):
-            v = var[:, c0:c1, :].rearrange("p c f -> p (c f)")
-            nc.vector.scalar_tensor_tensor(
-                out=v,
-                in0=lnq[:, c0:c1, :].rearrange("p c f -> p (c f)"),
-                scalar=-1.0 / M,
-                in1=a2_all[:, c0:c1, :].rearrange("p c f -> p (c f)"),
-                op0=ALU.mult,
-                op1=ALU.add,
-            )
-            nc.vector.tensor_scalar(out=v, in0=v, scalar1=0.0, scalar2=EPS, op0=ALU.max, op1=ALU.add)
-            for c in range(c0, c1):
-                nc.sync.dma_start(
-                    out=out_1[c * CH : (c + 1) * CH, :].rearrange("(p r) o -> p (r o)", r=R), in_=var[:, c, :]
+                nc.vector.scalar_tensor_tensor(
+                    out=q[:, pr, :], in0=pair[k]["sg"][:], scalar=DELTA, in1=q[:, pr, :], op0=ALU.max, op1=ALU.mult
                 )
 
-        load_w(0)
-        load_x(0)
+        def mean_of(pr):
+            nc.scalar.activation(
+                out=mean_p[:, pr, :], in_=group[pr][:], func=ACT.Identity, bias=mean_bias[:], scale=1.0 / M
+            )
+
+        def mean_square(pr):
+            nc.scalar.activation(
+                out=msq[:, pr, :], in_=group[pr][:], func=ACT.Square, bias=mean_bias[:], scale=1.0 / M
+            )
+
+        def spread_of(pr):
+            nc.vector.scalar_tensor_tensor(
+                out=spread[:, pr, :], in0=acc[:, pr, :], scalar=1.0 / M, in1=msq[:, pr, :], op0=ALU.mult, op1=ALU.subtract
+            )
+
+        def log_of(pr):
+            nc.scalar.activation(out=lnq[:, pr, :], in_=q[:, pr, :], func=ACT.Ln, scale=LN_SCALE)
+
+        def variance_of(pr):
+            nc.vector.scalar_tensor_tensor(
+                out=var_p[:, pr, :], in0=lnq[:, pr, :], scalar=-1.0 / M, in1=spread[:, pr, :], op0=ALU.mult, op1=ALU.add
+            )
+            nc.vector.tensor_scalar(
+                out=var_p[:, pr, :], in0=var_p[:, pr, :], scalar1=shift[:, 0:1], scalar2=EPS, op0=ALU.add, op1=ALU.max
+            )
+
+        def turn(src, pr):
+            bank = psum.tile([P, R, P], F32, tag="bank", name="turned_bank")
+            for r in range(R):
+                nc.tensor.transpose(bank[:, r, :], src[:, pr, r * P : (r + 1) * P], ident[:])
+            return bank
+
+        def store(copy, bank, out, pr):
+            result = epi.tile([P, 2, R, O], F32, tag="result")
+            copy(out=result[:], in_=bank[:].rearrange("p r (h o) -> p h r o", h=2))
+            nc.sync.dma_start(
+                out=out[pr * 2 * CH : (pr + 1) * 2 * CH, :].rearrange("(h p r) o -> p h (r o)", h=2, r=R),
+                in_=result[:].rearrange("p h r o -> p h (r o)"),
+            )
+
+        on_scalar = nc.scalar.copy
+        on_vector = nc.vector.tensor_copy
+
         setup()
+        load_w2(0, 2)
+        load_x(0, 2)
+        load_w3(0)
         load_x(1)
+        load_w2(1)
         load_x(2)
-        for i in range(-2, NU):
-            if i >= -1:
-                load_x(i + 4)
-            if i == 0:
-                load_bias3()
-            if i == -2:
-                load_w(1)
-            elif i % NCH == 1 and i // NCH + 2 < M:
-                load_w(i // NCH + 2)
-            piece = (i // NCH + 1, i % NCH) if (i >= 0 and i % NCH < 3 and i // NCH + 1 < M) else None
-            done = (i - 2) % NCH if (valid(i - 2) and (i - 2) // NCH == M - 1) else -1
-            add_bias3(i - 2)
-            x_exit(i + 1, 0)
-            x_exit(i + 1, 1)
-            if i == -2:
-                for j in range(3):
-                    w_transposes(0, j)
-                    w_exit(0, j)
-            x_transposes(i + 2, 0)
-            x_transposes(i + 2, 1)
-            if piece:
-                w_transposes(piece[0], piece[1])
-            if i < 1:
-                idle_plain(1)
-            hold_clock(i - 1, 2)
+        load_w3(1)
+        load_x(3)
+
+        w2_transposes(0, 0)
+        w2_transposes(0, 1)
+        w2_exit(0, 0, on_vector)
+        w2_exit(0, 1, on_scalar)
+        bias3_twice()
+        w2_quantise(0)
+        bias2()
+        x_transposes(0)
+        w3_transposes(0)
+        x_exit(0, 0, on_scalar)
+        x_exit(0, 1, on_vector)
+        quantise1(0)
+        w3_exit(0)
+        bias3_turn()
+        x_transposes(1)
+        for t in range(4):
+            layer1(0, t)
+        w3_quantise(0)
+        bias3()
+        load_w2(2)
+        load_w3(2)
+        w2_transposes(1, 0)
+        w2_transposes(1, 1)
+
+        for i in range(NU + 1):
+            even = i % 2 == 0
+            k = (i - 4) // 2 if even else (i - 3) // 2
+            n = i // 2 + 1 if even else (i + 3) // 2
+            shared = i >= 2 * M and i % 4 != 0 or i == 0
+            load_x(i + 4)
+            if even and n + 2 < M:
+                load_w2(n + 2)
+                load_w3(n + 2)
+            if even:
+                head_passes(k, 1)
+                mean_pass(k, 0)
+                mean_pass(k, 1)
+            else:
+                head_passes(k, 0)
+            x_exit(i + 1, 0, on_scalar)
+            x_exit(i + 1, 1, on_vector if i == 0 else on_scalar)
+            if even and n < M:
+                w2_exit(n, 0, on_vector)
+                w2_exit(n, 1, on_vector if n % 2 else on_scalar)
+            for t in range(3 if shared else 4):
+                h2_exit(i, t)
+                if t == 1:
+                    if even:
+                        sigmoid_raw(k)
+                    else:
+                        square_means(k)
+            if not even and i // 2 + 1 < M:
+                w3_exit(i // 2 + 1)
             regroup(i - 1)
             quantise1(i + 1)
-            if done >= 0:
-                mean_of(done)
-            h2_exit(i, 0)
-            if piece:
-                w_exit(piece[0], piece[1])
-                if piece[1] == 2:
-                    w_quantise(piece[0])
-            if i == -2:
-                w_quantise(0)
-                bias2()
-            if i == 1:
-                bias3()
-            nonlinear(i - 2)
-            if done >= 0:
-                mean_square(done)
-            layer1(i + 1, 0)
-            h2_exit(i, 1)
-            layer1(i + 1, 1)
+            if shared:
+                h2_exit(i, 3, True)
+            if even:
+                add_excess(k)
+            else:
+                multiply_sigmoid((i - 5) // 2)
             quantise2(i - 1)
-            layer2(i - 1)
-            accumulate(i - 2)
-            if done >= 0:
-                spread_sum(done)
-                spread_of(done)
-            h2_exit(i, 2)
-            layer1(i + 1, 2)
-            h2_exit(i, 3)
-            layer1(i + 1, 3)
-        last = NU - 1
-        hold_clock(last, 3)
-        regroup(last)
-        quantise2(last)
-        add_bias3(last - 1)
-        mean_of(NCH - 2)
-        layer2(last)
-        nonlinear(last - 1)
-        mean_square(NCH - 2)
-        add_bias3(last)
-        nonlinear(last)
-        accumulate(last - 1)
-        log_of(0, NCH - 2)
-        spread_sum(NCH - 2)
-        spread_of(NCH - 2)
-        accumulate(last)
-        mean_of(NCH - 1)
-        spread_sum(NCH - 1)
-        mean_square(NCH - 1)
-        log_of(NCH - 2, NCH)
-        variance_of(0, NCH - 2)
-        spread_of(NCH - 1)
-        variance_of(NCH - 2, NCH)
+            if even:
+                add_squares(k)
+                if n < M:
+                    w2_quantise(n)
+            else:
+                if i // 2 + 1 < M:
+                    w3_quantise(i // 2 + 1)
+            if i == 2 * M + 3:
+                spread_of(0)
+                store(on_scalar, turn(mean_p, 0), out_0, 0)
+            x_transposes(i + 2)
+            if even and n < M:
+                w3_transposes(n)
+            if not even and n < M:
+                w2_transposes(n, 0)
+                w2_transposes(n, 1)
+            for t in range(4):
+                layer1(i + 1, t)
+            if i == 2 * M + 2:
+                mean_of(0)
+                mean_square(0)
+
+        z = NK - 1
+        multiply_sigmoid(z - 1)
+        head_bank(z, 1, "bank", 6)
+        head_bank(z, 0, "bank", 6)
+        for h in range(2):
+            head_pass(z, 1, h)
+            head_pass(z, 0, h)
+            mean_pass(z, h)
+        sigmoid_raw(z)
+        square_means(z)
+        mean_square(1)
+        multiply_sigmoid(z)
+        add_squares(z)
+        add_excess(z)
+        spread_of(1)
+        log_of(0)
+        log_of(1)
+        variance_of(0)
+        mean_of(1)
+        variance_of(1)
+        store(on_scalar, turn(mean_p, 1), out_0, 1)
+        store(on_scalar, turn(var_p, 0), out_1, 0)
+        store(on_vector, turn(var_p, 1), out_1, 1)

@@ -106,7 +106,8 @@ def tile_gaussianmixturemlp_pa_kernel(tc, h1, W2, b2, W3, b3, out_0, out_1):
             nc.vector.tensor_copy(out=b2f[:], in_=b2raw[:])
 
         def bias3_twice():
-            nc.vector.tensor_copy(out=identb[:], in_=ident[:, 0:8])
+            nc.vector.tensor_copy(out=identb[:, 0:M], in_=ident[:, 0:M])
+            nc.vector.memset(identb[:, M:8], 1.0)
             nc.vector.tensor_copy(out=b3twice[:], in_=b3rows[:].unsqueeze(2).to_broadcast([P, 2, 2, O]))
 
         def bias3_turn():
@@ -120,14 +121,19 @@ def tile_gaussianmixturemlp_pa_kernel(tc, h1, W2, b2, W3, b3, out_0, out_1):
 
         def bias3():
             nc.vector.tensor_copy(out=b3cols[:], in_=group["turned"][:])
-            nc.vector.tensor_scalar_mul(out=neg_raw[:], in0=b3cols[:, 1, 0:M], scalar1=-1.0)
-            nc.vector.tensor_reduce(out=mean_bias[:], in_=b3cols[:, 0, 0:M], axis=mybir.AxisListType.X, op=ALU.add)
-            nc.vector.tensor_scalar_add(out=edge[:], in0=neg_raw[:], scalar1=CLAMP)
-            nc.vector.tensor_scalar_mul(out=mean_bias[:], in0=mean_bias[:], scalar1=1.0 / M)
-            nc.vector.tensor_reduce(out=shift[:], in_=edge[:], axis=mybir.AxisListType.X, op=ALU.add)
-            nc.vector.tensor_scalar(
-                out=shift[:], in0=shift[:], scalar1=-1.0 / M, scalar2=math.log(LN_SCALE) / M + 2 * EPS,
-                op0=ALU.mult, op1=ALU.add,
+            means, raws = b3cols[:, 0, :], b3cols[:, 1, :]
+            nc.gpsimd.tensor_scalar(
+                out=neg_raw[:], in0=raws[:, 0:M], scalar1=-1.0, scalar2=0.0, op0=ALU.mult, op1=ALU.add
+            )
+            nc.gpsimd.tensor_scalar(
+                out=edge[:], in0=raws[:, 0:M], scalar1=-1.0, scalar2=CLAMP, op0=ALU.mult, op1=ALU.add
+            )
+            nc.gpsimd.tensor_scalar(
+                out=mean_bias[:], in0=means[:, M : M + 1], scalar1=1.0 / M, scalar2=0.0, op0=ALU.mult, op1=ALU.add
+            )
+            nc.gpsimd.tensor_scalar(
+                out=shift[:], in0=raws[:, M : M + 1], scalar1=1.0 / M,
+                scalar2=math.log(LN_SCALE) / M - CLAMP + 2 * EPS, op0=ALU.mult, op1=ALU.add,
             )
 
         def load_w2(m, pieces=1):
@@ -177,12 +183,16 @@ def tile_gaussianmixturemlp_pa_kernel(tc, h1, W2, b2, W3, b3, out_0, out_1):
 
         def w2_exit(m, j, copy):
             d = wt[m]
-            if j == 0:
+            if "gw2" not in d:
                 d["gw2"] = work.tile([P, 4 * H], BF16, align_bytes=64, tag="gw2", bufs=2, name="gw2")
             words_out(copy, d["gw2"], j, d["tp%d" % j])
 
-        def w2_quantise(m):
-            nc.vector.quantize_mx(out=w2c[:, m, :].bitcast(FP8X4), scales=w2s[:, m, :], in_=wt[m]["gw2"][:])
+        def w2_quantise(m, j=None):
+            cols = slice(0, H) if j is None else slice(2 * j * P, 2 * (j + 1) * P)
+            raw = slice(4 * cols.start, 4 * cols.stop)
+            nc.vector.quantize_mx(
+                out=w2c[:, m, cols].bitcast(FP8X4), scales=w2s[:, m, cols], in_=wt[m]["gw2"][:, raw]
+            )
 
         def w3_transposes(m):
             d = wt[m]
@@ -380,15 +390,15 @@ def tile_gaussianmixturemlp_pa_kernel(tc, h1, W2, b2, W3, b3, out_0, out_1):
                 out=spread[:, pr, :], in0=acc[:, pr, :], scalar=1.0 / M, in1=msq[:, pr, :], op0=ALU.mult, op1=ALU.subtract
             )
 
+        def shift_spread(pr):
+            nc.vector.tensor_scalar_add(out=spread[:, pr, :], in0=spread[:, pr, :], scalar1=shift[:, 0:1])
+
         def log_of(pr):
             nc.scalar.activation(out=lnq[:, pr, :], in_=q[:, pr, :], func=ACT.Ln, scale=LN_SCALE)
 
         def variance_of(pr):
             nc.vector.scalar_tensor_tensor(
                 out=var_p[:, pr, :], in0=lnq[:, pr, :], scalar=-1.0 / M, in1=spread[:, pr, :], op0=ALU.mult, op1=ALU.add
-            )
-            nc.vector.tensor_scalar(
-                out=var_p[:, pr, :], in0=var_p[:, pr, :], scalar1=shift[:, 0:1], scalar2=EPS, op0=ALU.add, op1=ALU.max
             )
 
         def turn(src, pr):
@@ -398,12 +408,15 @@ def tile_gaussianmixturemlp_pa_kernel(tc, h1, W2, b2, W3, b3, out_0, out_1):
             return bank
 
         def store(copy, bank, out, pr):
-            result = epi.tile([P, 2, R, O], F32, tag="result")
+            result = epi.tile([P, 2, R, O], F32, tag="result", bufs=4)
             copy(out=result[:], in_=bank[:].rearrange("p r (h o) -> p h r o", h=2))
             nc.sync.dma_start(
                 out=out[pr * 2 * CH : (pr + 1) * 2 * CH, :].rearrange("(h p r) o -> p h (r o)", h=2, r=R),
                 in_=result[:].rearrange("p h r o -> p h (r o)"),
             )
+
+        def floored(out, in_):
+            nc.vector.tensor_scalar_max(out=out, in0=in_, scalar1=EPS)
 
         on_scalar = nc.scalar.copy
         on_vector = nc.vector.tensor_copy
@@ -411,46 +424,43 @@ def tile_gaussianmixturemlp_pa_kernel(tc, h1, W2, b2, W3, b3, out_0, out_1):
         setup()
         load_w2(0, 2)
         load_x(0, 2)
-        load_w3(0)
         load_x(1)
-        load_w2(1)
         load_x(2)
-        load_w3(1)
+        load_w2(1)
+        load_w3(0)
         load_x(3)
+        load_w2(2)
+        load_w3(1)
 
         w2_transposes(0, 0)
         w2_transposes(0, 1)
         w2_exit(0, 0, on_vector)
         w2_exit(0, 1, on_scalar)
-        bias3_twice()
-        w2_quantise(0)
+        w2_quantise(0, 0)
         bias2()
+        w2_quantise(0, 1)
         x_transposes(0)
-        w3_transposes(0)
         x_exit(0, 0, on_scalar)
         x_exit(0, 1, on_vector)
         quantise1(0)
-        w3_exit(0)
-        bias3_turn()
         x_transposes(1)
         for t in range(4):
             layer1(0, t)
-        w3_quantise(0)
-        bias3()
-        load_w2(2)
-        load_w3(2)
-        w2_transposes(1, 0)
-        w2_transposes(1, 1)
 
-        for i in range(NU + 1):
+        for i in range(NU):
             even = i % 2 == 0
             k = (i - 4) // 2 if even else (i - 3) // 2
-            n = i // 2 + 1 if even else (i + 3) // 2
-            shared = i >= 2 * M and i % 4 != 0 or i == 0
+            shared = i >= 2 * M - 2 and i % 4 != 0 and i != NU - 2 or i == 0
+            late = i == 0
+            turns2 = [(1, 0), (1, 1)] if i == 0 else [(n, j) for n in range(2, M) for j in range(2) if 2 * n - 3 + j == i]
+            exits2 = [(1, 0), (1, 1)] if i == 1 else [(n, j) for n in range(2, M) for j in range(2) if 2 * n - 2 + j == i]
+            turns3 = [n for n in range(M) if 2 * n == i]
+            exits3 = [n for n in range(M) if 2 * n + 1 == i]
             load_x(i + 4)
-            if even and n + 2 < M:
-                load_w2(n + 2)
-                load_w3(n + 2)
+            if not even and (i + 5) // 2 < M:
+                load_w2((i + 5) // 2)
+            if not even and (i + 3) // 2 < M:
+                load_w3((i + 3) // 2)
             if even:
                 head_passes(k, 1)
                 mean_pass(k, 0)
@@ -458,23 +468,38 @@ def tile_gaussianmixturemlp_pa_kernel(tc, h1, W2, b2, W3, b3, out_0, out_1):
             else:
                 head_passes(k, 0)
             x_exit(i + 1, 0, on_scalar)
-            x_exit(i + 1, 1, on_vector if i == 0 else on_scalar)
-            if even and n < M:
-                w2_exit(n, 0, on_vector)
-                w2_exit(n, 1, on_vector if n % 2 else on_scalar)
+            x_exit(i + 1, 1, on_vector if i <= 1 else on_scalar)
             for t in range(3 if shared else 4):
                 h2_exit(i, t)
+                for n, j in exits2:
+                    if j == 1 and n % 2 == 1 and t == (2 if i == 1 else 0):
+                        w2_exit(n, j, on_scalar)
                 if t == 1:
                     if even:
                         sigmoid_raw(k)
                     else:
                         square_means(k)
-            if not even and i // 2 + 1 < M:
-                w3_exit(i // 2 + 1)
-            regroup(i - 1)
-            quantise1(i + 1)
-            if shared:
+            if i <= 1:
+                regroup(i - 1)
+                quantise1(i + 1)
+            if i == 1:
+                bias3()
+            for n, j in exits2:
+                if j == 0 or n % 2 == 0:
+                    w2_exit(n, j, on_vector)
+            for n in exits3:
+                w3_exit(n)
+            if i == NU - 1:
                 h2_exit(i, 3, True)
+            if i > 1:
+                regroup(i - 1)
+                quantise1(i + 1)
+            for n, j in exits2:
+                w2_quantise(n, j)
+            if shared and i < NU - 1:
+                h2_exit(i, 3, True)
+            if i == 0:
+                bias3_twice()
             if even:
                 add_excess(k)
             else:
@@ -482,34 +507,49 @@ def tile_gaussianmixturemlp_pa_kernel(tc, h1, W2, b2, W3, b3, out_0, out_1):
             quantise2(i - 1)
             if even:
                 add_squares(k)
-                if n < M:
-                    w2_quantise(n)
-            else:
-                if i // 2 + 1 < M:
-                    w3_quantise(i // 2 + 1)
+            for n in exits3:
+                w3_quantise(n)
             if i == 2 * M + 3:
                 spread_of(0)
                 store(on_scalar, turn(mean_p, 0), out_0, 0)
+                shift_spread(0)
             x_transposes(i + 2)
-            if even and n < M:
-                w3_transposes(n)
-            if not even and n < M:
-                w2_transposes(n, 0)
-                w2_transposes(n, 1)
+            if not late:
+                for n, j in turns2:
+                    w2_transposes(n, j)
+                for n in turns3:
+                    w3_transposes(n)
             for t in range(4):
                 layer1(i + 1, t)
+            if late:
+                bias3_turn()
+                for n, j in turns2:
+                    w2_transposes(n, j)
+                for n in turns3:
+                    w3_transposes(n)
             if i == 2 * M + 2:
                 mean_of(0)
                 mean_square(0)
 
         z = NK - 1
-        multiply_sigmoid(z - 1)
+        last = NU - 1
+        head_passes(z - 1, 1)
+        mean_pass(z - 1, 0)
+        mean_pass(z - 1, 1)
+        sigmoid_raw(z - 1)
         head_bank(z, 1, "bank", 6)
         head_bank(z, 0, "bank", 6)
-        for h in range(2):
-            head_pass(z, 1, h)
-            head_pass(z, 0, h)
-            mean_pass(z, h)
+        head_pass(z, 1, 0)
+        head_pass(z, 0, 0)
+        mean_pass(z, 0)
+        regroup(last)
+        quantise2(last)
+        multiply_sigmoid(z - 1)
+        add_excess(z - 1)
+        add_squares(z - 1)
+        head_pass(z, 1, 1)
+        head_pass(z, 0, 1)
+        mean_pass(z, 1)
         sigmoid_raw(z)
         square_means(z)
         mean_square(1)
@@ -517,11 +557,12 @@ def tile_gaussianmixturemlp_pa_kernel(tc, h1, W2, b2, W3, b3, out_0, out_1):
         add_squares(z)
         add_excess(z)
         spread_of(1)
-        log_of(0)
-        log_of(1)
-        variance_of(0)
+        shift_spread(1)
         mean_of(1)
+        log_of(1)
+        log_of(0)
         variance_of(1)
+        variance_of(0)
         store(on_scalar, turn(mean_p, 1), out_0, 1)
-        store(on_scalar, turn(var_p, 0), out_1, 0)
-        store(on_vector, turn(var_p, 1), out_1, 1)
+        store(floored, turn(var_p, 1), out_1, 1)
+        store(floored, turn(var_p, 0), out_1, 0)

@@ -57,6 +57,7 @@ def tile_gaussianmixturemlp_pa_kernel(tc, h1, W2, b2, W3, b3, out_0, out_1):
         neg_raw = const.tile([P, M], F32)
         edge = const.tile([P, M], F32)
         mean_bias = const.tile([P, 1], F32)
+        root_bias = const.tile([P, 1], F32)
         shift = const.tile([P, 1], F32)
         zeros = const.tile([P, CH], BF16)
 
@@ -132,19 +133,19 @@ def tile_gaussianmixturemlp_pa_kernel(tc, h1, W2, b2, W3, b3, out_0, out_1):
                 out=mean_bias[:], in0=means[:, M : M + 1], scalar1=1.0 / M, scalar2=0.0, op0=ALU.mult, op1=ALU.add
             )
             nc.gpsimd.tensor_scalar(
-                out=shift[:], in0=raws[:, M : M + 1], scalar1=1.0 / M,
-                scalar2=math.log(LN_SCALE) / M - CLAMP + 2 * EPS, op0=ALU.mult, op1=ALU.add,
+                out=root_bias[:], in0=means[:, M : M + 1], scalar1=1.0 / math.sqrt(M), scalar2=0.0, op0=ALU.mult, op1=ALU.add
+            )
+            nc.gpsimd.tensor_scalar(
+                out=shift[:], in0=raws[:, M : M + 1], scalar1=1.0,
+                scalar2=math.log(LN_SCALE) + M * (2 * EPS - CLAMP), op0=ALU.mult, op1=ALU.add,
             )
 
-        def load_w2(m, pieces=1):
-            w2raw = wraw.tile([P, 4 * H], BF16, tag="w2raw")
-            n = 4 * H // pieces
-            for j in range(pieces):
-                nc.sync.dma_start(
-                    out=w2raw[:, j * n : (j + 1) * n],
-                    in_=W2[m].rearrange("(p t) k -> p (t k)", t=4)[:, j * n : (j + 1) * n],
-                )
-            wt.setdefault(m, {})["w2raw"] = w2raw
+        def load_w2(m, j=None):
+            d = wt.setdefault(m, {})
+            if "w2raw" not in d:
+                d["w2raw"] = wraw.tile([P, 4 * H], BF16, tag="w2raw", name="w2raw")
+            cols = slice(0, 4 * H) if j is None else slice(2 * j * H, 2 * (j + 1) * H)
+            nc.sync.dma_start(out=d["w2raw"][:, cols], in_=W2[m].rearrange("(p t) k -> p (t k)", t=4)[:, cols])
 
         def load_w3(m):
             w3raw = wraw.tile([P, H], BF16, tag="w3raw")
@@ -382,24 +383,19 @@ def tile_gaussianmixturemlp_pa_kernel(tc, h1, W2, b2, W3, b3, out_0, out_1):
 
         def mean_square(pr):
             nc.scalar.activation(
-                out=msq[:, pr, :], in_=group[pr][:], func=ACT.Square, bias=mean_bias[:], scale=1.0 / M
+                out=msq[:, pr, :], in_=group[pr][:], func=ACT.Square, bias=root_bias[:], scale=1.0 / math.sqrt(M)
             )
 
         def spread_of(pr):
             nc.vector.scalar_tensor_tensor(
-                out=spread[:, pr, :], in0=acc[:, pr, :], scalar=1.0 / M, in1=msq[:, pr, :], op0=ALU.mult, op1=ALU.subtract
+                out=spread[:, pr, :], in0=acc[:, pr, :], scalar=shift[:, 0:1], in1=msq[:, pr, :], op0=ALU.add, op1=ALU.subtract
             )
-
-        def shift_spread(pr):
-            nc.vector.tensor_scalar_add(out=spread[:, pr, :], in0=spread[:, pr, :], scalar1=shift[:, 0:1])
 
         def log_of(pr):
             nc.scalar.activation(out=lnq[:, pr, :], in_=q[:, pr, :], func=ACT.Ln, scale=LN_SCALE)
 
         def variance_of(pr):
-            nc.vector.scalar_tensor_tensor(
-                out=var_p[:, pr, :], in0=lnq[:, pr, :], scalar=-1.0 / M, in1=spread[:, pr, :], op0=ALU.mult, op1=ALU.add
-            )
+            nc.vector.tensor_tensor(out=var_p[:, pr, :], in0=spread[:, pr, :], in1=lnq[:, pr, :], op=ALU.subtract)
 
         def turn(src, pr):
             bank = psum.tile([P, R, P], F32, tag="bank", name="turned_bank")
@@ -416,14 +412,15 @@ def tile_gaussianmixturemlp_pa_kernel(tc, h1, W2, b2, W3, b3, out_0, out_1):
             )
 
         def floored(out, in_):
-            nc.vector.tensor_scalar_max(out=out, in0=in_, scalar1=EPS)
+            nc.vector.tensor_scalar(out=out, in0=in_, scalar1=1.0 / M, scalar2=EPS, op0=ALU.mult, op1=ALU.max)
 
         on_scalar = nc.scalar.copy
         on_vector = nc.vector.tensor_copy
 
         setup()
-        load_w2(0, 2)
+        load_w2(0, 0)
         load_x(0, 2)
+        load_w2(0, 1)
         load_x(1)
         load_x(2)
         load_w2(1)
@@ -433,16 +430,16 @@ def tile_gaussianmixturemlp_pa_kernel(tc, h1, W2, b2, W3, b3, out_0, out_1):
         load_w3(1)
 
         w2_transposes(0, 0)
-        w2_transposes(0, 1)
         w2_exit(0, 0, on_vector)
-        w2_exit(0, 1, on_scalar)
-        w2_quantise(0, 0)
-        bias2()
-        w2_quantise(0, 1)
         x_transposes(0)
         x_exit(0, 0, on_scalar)
+        w2_transposes(0, 1)
+        w2_quantise(0, 0)
         x_exit(0, 1, on_vector)
+        w2_exit(0, 1, on_scalar)
         quantise1(0)
+        w2_quantise(0, 1)
+        bias2()
         x_transposes(1)
         for t in range(4):
             layer1(0, t)
@@ -512,7 +509,6 @@ def tile_gaussianmixturemlp_pa_kernel(tc, h1, W2, b2, W3, b3, out_0, out_1):
             if i == 2 * M + 3:
                 spread_of(0)
                 store(on_scalar, turn(mean_p, 0), out_0, 0)
-                shift_spread(0)
             x_transposes(i + 2)
             if not late:
                 for n, j in turns2:
@@ -557,12 +553,11 @@ def tile_gaussianmixturemlp_pa_kernel(tc, h1, W2, b2, W3, b3, out_0, out_1):
         add_squares(z)
         add_excess(z)
         spread_of(1)
-        shift_spread(1)
-        mean_of(1)
-        log_of(1)
         log_of(0)
-        variance_of(1)
+        log_of(1)
+        mean_of(1)
         variance_of(0)
-        store(on_scalar, turn(mean_p, 1), out_0, 1)
-        store(floored, turn(var_p, 1), out_1, 1)
+        variance_of(1)
         store(floored, turn(var_p, 0), out_1, 0)
+        store(floored, turn(var_p, 1), out_1, 1)
+        store(on_scalar, turn(mean_p, 1), out_0, 1)

@@ -47,6 +47,7 @@ def tile_gaussianmixturemlp_pa_kernel(tc, h1, W2, b2, W3, b3, out_0, out_1):
 
         ident = const.tile([P, P], F32)
         identb = const.tile([P, 8], BF16)
+        ident16 = const.tile([P, P], BF16)
         ones = const.tile([P, 1], F32)
         table_warm = const.tile([P, 1], F32)
         b2raw = const.tile([P, M, 4], BF16)
@@ -98,6 +99,7 @@ def tile_gaussianmixturemlp_pa_kernel(tc, h1, W2, b2, W3, b3, out_0, out_1):
             nc.vector.memset(zeros[:], 0.0)
             idle_plain(4)
             make_identity(nc, ident[:])
+            nc.vector.tensor_copy(out=ident16[:], in_=ident[:])
             nc.vector.memset(ones[:], 1.0)
             nc.vector.memset(w3c[:], 0)
             nc.vector.memset(w3s[:].rearrange("p m w -> p (m w)").bitcast(U32), 0)
@@ -180,13 +182,22 @@ def tile_gaussianmixturemlp_pa_kernel(tc, h1, W2, b2, W3, b3, out_0, out_1):
 
         def w2_transposes(m, j):
             d = wt[m]
-            d["tp%d" % j] = transpose_pair(d["w2raw"][:].bitcast(F32), j)
+            bank = psum.tile([P, 2, 4, P], BF16, tag="bank", name="turned_w2")
+            for a in range(2):
+                for t in range(4):
+                    first = (2 * j + a) * H + t
+                    nc.tensor.matmul(
+                        out=bank[:, a, t, :], lhsT=d["w2raw"][:, first : first + H - 3 : 4], rhs=ident16[:],
+                        start=True, stop=True,
+                    )
+            d["tp%d" % j] = bank
 
         def w2_exit(m, j, copy):
             d = wt[m]
             if "gw2" not in d:
                 d["gw2"] = work.tile([P, 4 * H], BF16, align_bytes=64, tag="gw2", bufs=2, name="gw2")
-            words_out(copy, d["gw2"], j, d["tp%d" % j])
+            dst = d["gw2"][:].rearrange("q (r c t) -> q r c t", c=P, t=4)
+            copy(out=dst[:, 2 * j : 2 * j + 2], in_=d["tp%d" % j][:].rearrange("q a t c -> q a c t"))
 
         def w2_quantise(m, j=None):
             cols = slice(0, H) if j is None else slice(2 * j * P, 2 * (j + 1) * P)

@@ -25,6 +25,7 @@ NU = NP * M * 2
 NK = NP * M
 WP = 320
 EPS = 1e-6
+MATMUL_TURNED = 1
 CLAMP = 14.0
 DELTA = 1.0 / (1.0 + math.exp(CLAMP))
 LN_SCALE = 2.0 ** 40
@@ -182,6 +183,9 @@ def tile_gaussianmixturemlp_pa_kernel(tc, h1, W2, b2, W3, b3, out_0, out_1):
 
         def w2_transposes(m, j):
             d = wt[m]
+            if m > MATMUL_TURNED:
+                d["tp%d" % j] = transpose_pair(d["w2raw"][:].bitcast(F32), j)
+                return
             bank = psum.tile([P, 2, 4, P], BF16, tag="bank", name="turned_w2")
             for a in range(2):
                 for t in range(4):
@@ -196,6 +200,9 @@ def tile_gaussianmixturemlp_pa_kernel(tc, h1, W2, b2, W3, b3, out_0, out_1):
             d = wt[m]
             if "gw2" not in d:
                 d["gw2"] = work.tile([P, 4 * H], BF16, align_bytes=64, tag="gw2", bufs=2, name="gw2")
+            if m > MATMUL_TURNED:
+                words_out(copy, d["gw2"], j, d["tp%d" % j])
+                return
             dst = d["gw2"][:].rearrange("q (r c t) -> q r c t", c=P, t=4)
             copy(out=dst[:, 2 * j : 2 * j + 2], in_=d["tp%d" % j][:].rearrange("q a t c -> q a c t"))
 
@@ -397,33 +404,60 @@ def tile_gaussianmixturemlp_pa_kernel(tc, h1, W2, b2, W3, b3, out_0, out_1):
                 out=msq[:, pr, :], in_=group[pr][:], func=ACT.Square, bias=root_bias[:], scale=1.0 / math.sqrt(M)
             )
 
+        def mean_on_vector(pr):
+            nc.vector.tensor_scalar(
+                out=mean_p[:, pr, :], in0=group[pr][:], scalar1=1.0 / M, scalar2=mean_bias[:, 0:1], op0=ALU.mult, op1=ALU.add
+            )
+
+        def square_on_vector(pr):
+            nc.vector.scalar_tensor_tensor(
+                out=msq[:, pr, :], in0=mean_p[:, pr, :], scalar=float(M), in1=mean_p[:, pr, :], op0=ALU.mult, op1=ALU.mult
+            )
+
         def spread_of(pr):
             nc.vector.scalar_tensor_tensor(
                 out=spread[:, pr, :], in0=acc[:, pr, :], scalar=shift[:, 0:1], in1=msq[:, pr, :], op0=ALU.add, op1=ALU.subtract
             )
 
-        def log_of(pr):
-            nc.scalar.activation(out=lnq[:, pr, :], in_=q[:, pr, :], func=ACT.Ln, scale=LN_SCALE)
-
-        def variance_of(pr):
-            nc.vector.tensor_tensor(out=var_p[:, pr, :], in0=spread[:, pr, :], in1=lnq[:, pr, :], op=ALU.subtract)
-
-        def turn(src, pr):
+        def turn(src, adds=()):
             bank = psum.tile([P, R, P], F32, tag="bank", name="turned_bank")
-            for r in range(R):
-                nc.tensor.transpose(bank[:, r, :], src[:, pr, r * P : (r + 1) * P], ident[:])
+            parts = [src] + list(adds)
+            for n, part in enumerate(parts):
+                for r in range(R):
+                    nc.tensor.matmul(
+                        out=bank[:, r, :], lhsT=part[:, r * P : (r + 1) * P], rhs=ident[:], is_transpose=True,
+                        start=n == 0 and r == 0, stop=n == len(parts) - 1 and r == R - 1,
+                    )
             return bank
 
-        def store(copy, bank, out, pr):
+        def log_of(pr):
+            bank = turn(q[:, pr, :])
+            nc.scalar.activation(
+                out=lnq[:, pr, :], in_=bank[:].rearrange("p r c -> p (r c)"), func=ACT.Ln, scale=LN_SCALE
+            )
+
+        def variance_of(pr, bank):
+            nc.vector.tensor_tensor(
+                out=var_p[:, pr, :], in0=bank[:].rearrange("p r c -> p (r c)"), in1=lnq[:, pr, :], op=ALU.subtract
+            )
+
+        def store(out, pr, fill):
             result = epi.tile([P, 2, R, O], F32, tag="result", bufs=4)
-            copy(out=result[:], in_=bank[:].rearrange("p r (h o) -> p h r o", h=2))
+            fill(result)
             nc.sync.dma_start(
                 out=out[pr * 2 * CH : (pr + 1) * 2 * CH, :].rearrange("(h p r) o -> p h (r o)", h=2, r=R),
                 in_=result[:].rearrange("p h r o -> p h (r o)"),
             )
 
-        def floored(out, in_):
-            nc.vector.tensor_scalar(out=out, in0=in_, scalar1=1.0 / M, scalar2=EPS, op0=ALU.mult, op1=ALU.max)
+        def mean_out(pr):
+            bank = turn(mean_p[:, pr, :])
+            store(out_0, pr, lambda result: nc.scalar.copy(
+                out=result[:], in_=bank[:].rearrange("p r (h o) -> p h r o", h=2)))
+
+        def variance_out(pr):
+            store(out_1, pr, lambda result: nc.vector.tensor_scalar(
+                out=result[:], in0=var_p[:, pr, :].rearrange("p (r h o) -> p h r o", r=R, h=2),
+                scalar1=1.0 / M, scalar2=EPS, op0=ALU.mult, op1=ALU.max))
 
         on_scalar = nc.scalar.copy
         on_vector = nc.vector.tensor_copy
@@ -519,7 +553,7 @@ def tile_gaussianmixturemlp_pa_kernel(tc, h1, W2, b2, W3, b3, out_0, out_1):
                 w3_quantise(n)
             if i == 2 * M + 3:
                 spread_of(0)
-                store(on_scalar, turn(mean_p, 0), out_0, 0)
+                mean_out(0)
             x_transposes(i + 2)
             if not late:
                 for n, j in turns2:
@@ -553,22 +587,22 @@ def tile_gaussianmixturemlp_pa_kernel(tc, h1, W2, b2, W3, b3, out_0, out_1):
         quantise2(last)
         multiply_sigmoid(z - 1)
         add_excess(z - 1)
-        add_squares(z - 1)
         head_pass(z, 1, 1)
         head_pass(z, 0, 1)
         mean_pass(z, 1)
         sigmoid_raw(z)
         square_means(z)
-        mean_square(1)
+        mean_on_vector(1)
         multiply_sigmoid(z)
-        add_squares(z)
         add_excess(z)
+        square_on_vector(1)
         spread_of(1)
+        spread0 = turn(spread[:, 0, :])
         log_of(0)
         log_of(1)
-        mean_of(1)
-        variance_of(0)
-        variance_of(1)
-        store(floored, turn(var_p, 0), out_1, 0)
-        store(floored, turn(var_p, 1), out_1, 1)
-        store(on_scalar, turn(mean_p, 1), out_0, 1)
+        spread1 = turn(pair[z - 1]["sq"], [pair[z]["sq"], spread[:, 1, :]])
+        variance_of(0, spread0)
+        variance_out(0)
+        variance_of(1, spread1)
+        variance_out(1)
+        mean_out(1)

@@ -23,9 +23,12 @@ R = CH // P
 NP = B // (2 * CH)
 NU = NP * M * 2
 NK = NP * M
+ROUNDS = [(g, m) for m in range(M - 2) for g in range(NP)] + [(g, m) for g in range(NP) for m in (M - 2, M - 1)]
+FIRST = [2 * min(k for k in range(NK) if ROUNDS[k][1] == m) for m in range(M)]
 WP = 320
 EPS = 1e-6
-MATMUL_TURNED = 1
+MATMUL_TURNED = 0
+KEPT_FROM = 2
 CLAMP = 14.0
 DELTA = 1.0 / (1.0 + math.exp(CLAMP))
 LN_SCALE = 2.0 ** 40
@@ -84,9 +87,7 @@ def tile_gaussianmixturemlp_pa_kernel(tc, h1, W2, b2, W3, b3, out_0, out_1):
             return 0 <= u < NU
 
         def place(u):
-            k, h = divmod(u, 2)
-            pr, m = divmod(k, M)
-            return pr, m, h
+            return ROUNDS[u // 2] + (u % 2,)
 
         def idle_plain(n):
             scratch = psum.tile([P, CH], F32, tag="head", bufs=1, name="scratch")
@@ -311,8 +312,8 @@ def tile_gaussianmixturemlp_pa_kernel(tc, h1, W2, b2, W3, b3, out_0, out_1):
             if not valid(u):
                 return
             d = unit[u]
-            c2 = codes.tile([P, CH], U32, align_bytes=64, tag="c2", bufs=6)
-            s2 = codes.tile([P, CH], U8, align_bytes=64, tag="s2", bufs=6)
+            c2 = codes.tile([P, CH], U32, align_bytes=64, tag="c2", bufs=NU)
+            s2 = codes.tile([P, CH], U8, align_bytes=64, tag="s2", bufs=NU)
             nc.vector.quantize_mx(out=c2[:].bitcast(FP8X4), scales=s2[:], in_=d["g2"][:])
             d["c2"] = c2
             d["s2"] = s2
@@ -346,30 +347,37 @@ def tile_gaussianmixturemlp_pa_kernel(tc, h1, W2, b2, W3, b3, out_0, out_1):
         def mean_pass(k, h):
             if not 0 <= k < NK:
                 return
-            pr, m = divmod(k, M)
+            pr, m = ROUNDS[k]
             if m == 0 and h == 0:
-                group[pr] = psum.tile([P, CH], F32, tag="mean", bufs=1, name="mean_sum")
+                tag, bufs = ("mean", 1) if pr == 0 else ("bank", 6)
+                group[pr] = psum.tile([P, CH], F32, tag=tag, bufs=bufs, name="mean_sum")
             layer2(group[pr][:], 2 * k + h, 0, m == 0 and h == 0, m == M - 1 and h == 1)
+
+        def mean_passes(*ks):
+            for k in ks:
+                for h in range(2):
+                    mean_pass(k, h)
 
         def square_means(k):
             if not 0 <= k < NK:
                 return
-            m = k % M
-            sq = epi.tile([P, CH], F32, tag="sq")
+            pr, m = ROUNDS[k]
+            tag, bufs = ("sq", 2) if m < KEPT_FROM else ("kept_sq", NP * (M - KEPT_FROM))
+            sq = epi.tile([P, CH], F32, tag=tag, bufs=bufs, name="sq")
             nc.scalar.activation(out=sq[:], in_=pair[k][0][:], func=ACT.Square, bias=b3cols[:, 0, m : m + 1], scale=1.0)
             pair[k]["sq"] = sq
 
         def add_squares(k):
             if not 0 <= k < NK:
                 return
-            pr, m = divmod(k, M)
-            if m > 0:
+            pr, m = ROUNDS[k]
+            if 0 < m < KEPT_FROM:
                 nc.vector.tensor_tensor(out=acc[:, pr, :], in0=pair[k]["sq"][:], in1=acc[:, pr, :], op=ALU.add)
 
         def sigmoid_raw(k):
             if not 0 <= k < NK:
                 return
-            m = k % M
+            pr, m = ROUNDS[k]
             sg = epi.tile([P, CH], F32, tag="sg")
             nc.scalar.activation(out=sg[:], in_=pair[k][1][:], func=ACT.Sigmoid, bias=neg_raw[:, m : m + 1], scale=-1.0)
             pair[k]["sg"] = sg
@@ -377,7 +385,7 @@ def tile_gaussianmixturemlp_pa_kernel(tc, h1, W2, b2, W3, b3, out_0, out_1):
         def add_excess(k):
             if not 0 <= k < NK:
                 return
-            pr, m = divmod(k, M)
+            pr, m = ROUNDS[k]
             other = pair[k]["sq"][:] if m == 0 else acc[:, pr, :]
             nc.vector.scalar_tensor_tensor(
                 out=acc[:, pr, :], in0=pair[k][1][:], scalar=edge[:, m : m + 1], in1=other, op0=ALU.max, op1=ALU.add
@@ -386,7 +394,7 @@ def tile_gaussianmixturemlp_pa_kernel(tc, h1, W2, b2, W3, b3, out_0, out_1):
         def multiply_sigmoid(k):
             if not 0 <= k < NK:
                 return
-            pr, m = divmod(k, M)
+            pr, m = ROUNDS[k]
             if m == 0:
                 nc.vector.tensor_scalar_max(out=q[:, pr, :], in0=pair[k]["sg"][:], scalar1=DELTA)
             else:
@@ -419,16 +427,24 @@ def tile_gaussianmixturemlp_pa_kernel(tc, h1, W2, b2, W3, b3, out_0, out_1):
                 out=spread[:, pr, :], in0=acc[:, pr, :], scalar=shift[:, 0:1], in1=msq[:, pr, :], op0=ALU.add, op1=ALU.subtract
             )
 
-        def turn(src, adds=()):
-            bank = psum.tile([P, R, P], F32, tag="bank", name="turned_bank")
-            parts = [src] + list(adds)
-            for n, part in enumerate(parts):
-                for r in range(R):
-                    nc.tensor.matmul(
-                        out=bank[:, r, :], lhsT=part[:, r * P : (r + 1) * P], rhs=ident[:], is_transpose=True,
-                        start=n == 0 and r == 0, stop=n == len(parts) - 1 and r == R - 1,
-                    )
+        def turn_bank():
+            return psum.tile([P, R, P], F32, tag="bank", name="turned_bank")
+
+        def turn_into(bank, part, first=True, final=True):
+            for r in range(R):
+                nc.tensor.matmul(
+                    out=bank[:, r, :], lhsT=part[:, r * P : (r + 1) * P], rhs=ident[:], is_transpose=True,
+                    start=first and r == 0, stop=final and r == R - 1,
+                )
+
+        def turn(part):
+            bank = turn_bank()
+            turn_into(bank, part)
             return bank
+
+        def turn_squares(bank, ks, first):
+            for k in ks:
+                turn_into(bank, pair[k]["sq"], first and k == ks[0], False)
 
         def log_of(pr):
             bank = turn(q[:, pr, :])
@@ -471,7 +487,6 @@ def tile_gaussianmixturemlp_pa_kernel(tc, h1, W2, b2, W3, b3, out_0, out_1):
         load_w2(1)
         load_w3(0)
         load_x(3)
-        load_w2(2)
         load_w3(1)
 
         w2_transposes(0, 0)
@@ -489,32 +504,32 @@ def tile_gaussianmixturemlp_pa_kernel(tc, h1, W2, b2, W3, b3, out_0, out_1):
         for t in range(4):
             layer1(0, t)
 
+        own = [[k for k in range(NK) if ROUNDS[k][0] == g] for g in range(NP)]
+
         for i in range(NU):
             even = i % 2 == 0
             k = (i - 4) // 2 if even else (i - 3) // 2
-            shared = i >= 2 * M - 2 and i % 4 != 0 and i != NU - 2 or i == 0
-            late = i == 0
-            turns2 = [(1, 0), (1, 1)] if i == 0 else [(n, j) for n in range(2, M) for j in range(2) if 2 * n - 3 + j == i]
-            exits2 = [(1, 0), (1, 1)] if i == 1 else [(n, j) for n in range(2, M) for j in range(2) if 2 * n - 2 + j == i]
-            turns3 = [n for n in range(M) if 2 * n == i]
-            exits3 = [n for n in range(M) if 2 * n + 1 == i]
+            shared = i % 2 == 1 or i <= 2
+            turns2 = [(n, j) for n in range(1, M) for j in range(2) if FIRST[n] - 3 + j == i]
+            exits2 = [(n, j) for n in range(1, M) for j in range(2) if FIRST[n] - 2 + j == i]
+            turns3 = [n for n in range(M) if max(1, FIRST[n] - 1) == i]
+            exits3 = [n for n in range(M) if max(1, FIRST[n] - 1) + 1 == i]
             load_x(i + 4)
-            if not even and (i + 5) // 2 < M:
-                load_w2((i + 5) // 2)
-            if not even and (i + 3) // 2 < M:
-                load_w3((i + 3) // 2)
-            if even:
-                head_passes(k, 1)
-                mean_pass(k, 0)
-                mean_pass(k, 1)
-            else:
-                head_passes(k, 0)
+            for n in range(2, M):
+                if max(1, FIRST[n] - 6) == i:
+                    load_w2(n)
+                    load_w3(n)
+            head_passes(k, 1 if even else 0)
+            if NU - 7 <= i < NU - 2:
+                mean_passes(own[0][i - NU + 7])
+            if i == NU - 1:
+                mean_passes(*own[1][:2])
             x_exit(i + 1, 0, on_scalar)
             x_exit(i + 1, 1, on_vector if i <= 1 else on_scalar)
             for t in range(3 if shared else 4):
                 h2_exit(i, t)
                 for n, j in exits2:
-                    if j == 1 and n % 2 == 1 and t == (2 if i == 1 else 0):
+                    if j == 1 and n % 2 == 1 and t == 0:
                         w2_exit(n, j, on_scalar)
                 if t == 1:
                     if even:
@@ -551,33 +566,25 @@ def tile_gaussianmixturemlp_pa_kernel(tc, h1, W2, b2, W3, b3, out_0, out_1):
                 add_squares(k)
             for n in exits3:
                 w3_quantise(n)
-            if i == 2 * M + 3:
-                spread_of(0)
-                mean_out(0)
             x_transposes(i + 2)
-            if not late:
-                for n, j in turns2:
-                    w2_transposes(n, j)
-                for n in turns3:
-                    w3_transposes(n)
+            for n, j in turns2:
+                w2_transposes(n, j)
+            for n in turns3:
+                w3_transposes(n)
             for t in range(4):
                 layer1(i + 1, t)
-            if late:
+            if i == 0:
                 bias3_turn()
-                for n, j in turns2:
-                    w2_transposes(n, j)
-                for n in turns3:
-                    w3_transposes(n)
-            if i == 2 * M + 2:
-                mean_of(0)
-                mean_square(0)
-
         z = NK - 1
         last = NU - 1
+        kept = [own[g][KEPT_FROM:] for g in range(NP)]
+        sums = [turn_bank() for g in range(NP)]
+        turn_squares(sums[0], kept[0], True)
         head_passes(z - 1, 1)
-        mean_pass(z - 1, 0)
-        mean_pass(z - 1, 1)
+        mean_passes(*own[1][2:4])
         sigmoid_raw(z - 1)
+        mean_of(0)
+        mean_square(0)
         head_bank(z, 1, "bank", 6)
         head_bank(z, 0, "bank", 6)
         head_pass(z, 1, 0)
@@ -595,14 +602,17 @@ def tile_gaussianmixturemlp_pa_kernel(tc, h1, W2, b2, W3, b3, out_0, out_1):
         mean_on_vector(1)
         multiply_sigmoid(z)
         add_excess(z)
+        spread_of(0)
         square_on_vector(1)
         spread_of(1)
-        spread0 = turn(spread[:, 0, :])
         log_of(0)
+        turn_squares(sums[1], kept[1], True)
+        turn_into(sums[0], spread[:, 0, :], False)
         log_of(1)
-        spread1 = turn(pair[z - 1]["sq"], [pair[z]["sq"], spread[:, 1, :]])
-        variance_of(0, spread0)
+        turn_into(sums[1], spread[:, 1, :], False)
+        variance_of(0, sums[0])
         variance_out(0)
-        variance_of(1, spread1)
+        variance_of(1, sums[1])
         variance_out(1)
+        mean_out(0)
         mean_out(1)

@@ -303,8 +303,8 @@ def tile_gaussianmixturemlp_pa_kernel(tc, h1, W2, b2, W3, b3, out_0, out_1):
             d = unit[u]
             g2 = work.tile([P, 4 * CH], BF16, align_bytes=64, tag="g2")
             nc.vector.tensor_copy(
-                out=g2[:].rearrange("p (c i t) -> p c t i", i=4, t=4),
-                in_=d["planes"][:].rearrange("p t (c i) -> p c t i", i=4),
+                out=g2[:].rearrange("p (c i t) -> p c t i", i=8, t=4),
+                in_=d["planes"][:].rearrange("p t (c i) -> p c t i", i=8),
             )
             d["g2"] = g2
 

@@ -66,10 +66,10 @@ def tile_gaussianmixturemlp_pa_kernel(tc, h1, W2, b2, W3, b3, out_0, out_1):
         shift = const.tile([P, 1], F32)
         zeros = const.tile([P, CH], BF16)
 
-        w2c = keep.tile([P, M, H], U32, align_bytes=64)
-        w2s = keep.tile([P, M, H], U8, align_bytes=64)
-        w3c = keep.tile([P, M, WP], U32, align_bytes=64)
-        w3s = keep.tile([P, M, WP], U8, align_bytes=64)
+        w2c = keep.tile([P, M, H], U32, align_bytes=256)
+        w2s = keep.tile([P, M, H], U8, align_bytes=256)
+        w3c = keep.tile([P, M, WP], U32, align_bytes=256)
+        w3s = keep.tile([P, M, WP], U8, align_bytes=256)
         q = keep.tile([P, NP, CH], F32)
         acc = keep.tile([P, NP, CH], F32)
         lnq = keep.tile([P, NP, CH], F32)
@@ -257,8 +257,8 @@ def tile_gaussianmixturemlp_pa_kernel(tc, h1, W2, b2, W3, b3, out_0, out_1):
             if not valid(u):
                 return
             d = unit[u]
-            c1 = codes.tile([P, CH], U32, align_bytes=64, tag="c1")
-            s1 = codes.tile([P, CH], U8, align_bytes=64, tag="s1")
+            c1 = codes.tile([P, CH], U32, align_bytes=256, tag="c1")
+            s1 = codes.tile([P, CH], U8, align_bytes=256, tag="s1")
             nc.vector.quantize_mx(out=c1[:].bitcast(FP8X4), scales=s1[:], in_=d["g1"][:])
             d["c1"] = c1
             d["s1"] = s1
@@ -312,8 +312,8 @@ def tile_gaussianmixturemlp_pa_kernel(tc, h1, W2, b2, W3, b3, out_0, out_1):
             if not valid(u):
                 return
             d = unit[u]
-            c2 = codes.tile([P, CH], U32, align_bytes=64, tag="c2", bufs=NU)
-            s2 = codes.tile([P, CH], U8, align_bytes=64, tag="s2", bufs=NU)
+            c2 = codes.tile([P, CH], U32, align_bytes=256, tag="c2", bufs=NU)
+            s2 = codes.tile([P, CH], U8, align_bytes=256, tag="s2", bufs=NU)
             nc.vector.quantize_mx(out=c2[:].bitcast(FP8X4), scales=s2[:], in_=d["g2"][:])
             d["c2"] = c2
             d["s2"] = s2

@@ -427,8 +427,8 @@ def tile_gaussianmixturemlp_pa_kernel(tc, h1, W2, b2, W3, b3, out_0, out_1):
                 out=spread[:, pr, :], in0=acc[:, pr, :], scalar=shift[:, 0:1], in1=msq[:, pr, :], op0=ALU.add, op1=ALU.subtract
             )
 
-        def turn_bank():
-            return psum.tile([P, R, P], F32, tag="bank", name="turned_bank")
+        def turn_bank(tag="bank", bufs=6):
+            return psum.tile([P, R, P], F32, tag=tag, bufs=bufs, name="turned_bank")
 
         def turn_into(bank, part, first=True, final=True):
             for r in range(R):
@@ -437,8 +437,8 @@ def tile_gaussianmixturemlp_pa_kernel(tc, h1, W2, b2, W3, b3, out_0, out_1):
                     start=first and r == 0, stop=final and r == R - 1,
                 )
 
-        def turn(part):
-            bank = turn_bank()
+        def turn(part, tag="bank", bufs=6):
+            bank = turn_bank(tag, bufs)
             turn_into(bank, part)
             return bank
 
@@ -466,7 +466,7 @@ def tile_gaussianmixturemlp_pa_kernel(tc, h1, W2, b2, W3, b3, out_0, out_1):
             )
 
         def mean_out(pr):
-            bank = turn(mean_p[:, pr, :])
+            bank = turn(mean_p[:, pr, :], "mean" if pr == 0 else "head", 1)
             store(out_0, pr, lambda result: nc.scalar.copy(
                 out=result[:], in_=bank[:].rearrange("p r (h o) -> p h r o", h=2)))
 
@@ -599,20 +599,21 @@ def tile_gaussianmixturemlp_pa_kernel(tc, h1, W2, b2, W3, b3, out_0, out_1):
         mean_pass(z, 1)
         sigmoid_raw(z)
         square_means(z)
+        spread_of(0)
         mean_on_vector(1)
         multiply_sigmoid(z)
         add_excess(z)
-        spread_of(0)
         square_on_vector(1)
         spread_of(1)
         log_of(0)
-        turn_squares(sums[1], kept[1], True)
         turn_into(sums[0], spread[:, 0, :], False)
+        turn_squares(sums[1], kept[1][:-1], True)
         log_of(1)
+        turn_squares(sums[1], kept[1][-1:], False)
+        mean_out(0)
+        mean_out(1)
         turn_into(sums[1], spread[:, 1, :], False)
         variance_of(0, sums[0])
         variance_out(0)
         variance_of(1, sums[1])
         variance_out(1)
-        mean_out(0)
-        mean_out(1)

import math
from contextlib import ExitStack

import concourse.mybir as mybir
from concourse.masks import make_identity

F32 = mybir.dt.float32
BF16 = mybir.dt.bfloat16
U32 = mybir.dt.uint32
U8 = mybir.dt.uint8
FP8X4 = mybir.dt.float8_e4m3fn_x4
ALU = mybir.AluOpType
ACT = mybir.ActivationFunctionType

P = 128
M = 5
B = 2048
H = 512
O = 64
O2 = 128
CH = 512
R = CH // P
NP = B // (2 * CH)
NU = NP * M * 2
NK = NP * M
ROUNDS = [(g, m) for m in range(M - 2) for g in range(NP)] + [(g, m) for g in range(NP) for m in (M - 2, M - 1)]
FIRST = [2 * min(k for k in range(NK) if ROUNDS[k][1] == m) for m in range(M)]
WP = 320
EPS = 1e-6
MATMUL_TURNED = 0
KEPT_FROM = 2
CLAMP = 14.0
DELTA = 1.0 / (1.0 + math.exp(CLAMP))
LN_SCALE = 2.0 ** 40

FLOPS = 2 * M * B * H * H + 2 * M * B * H * O2


def tile_gaussianmixturemlp_pa_kernel(tc, h1, W2, b2, W3, b3, out_0, out_1):
    nc = tc.nc
    with ExitStack() as ctx:
        const = ctx.enter_context(tc.tile_pool(name="const", bufs=1))
        keep = ctx.enter_context(tc.tile_pool(name="keep", bufs=1))
        wraw = ctx.enter_context(tc.tile_pool(name="wraw", bufs=2))
        xin = ctx.enter_context(tc.tile_pool(name="xin", bufs=5))
        work = ctx.enter_context(tc.tile_pool(name="work", bufs=3))
        codes = ctx.enter_context(tc.tile_pool(name="codes", bufs=3))
        epi = ctx.enter_context(tc.tile_pool(name="epi", bufs=2))
        psum = ctx.enter_context(tc.psum_pool(name="psum", bufs=6))
        ctx.enter_context(tc.manual_schedule())

        ident = const.tile([P, P], F32)
        identb = const.tile([P, 8], BF16)
        ident16 = const.tile([P, P], BF16)
        ones = const.tile([P, 1], F32)
        table_warm = const.tile([P, 1], F32)
        b2raw = const.tile([P, M, 4], BF16)
        b2f = const.tile([P, M, 4], F32)
        b3rows = const.tile([P, 2, O], BF16)
        b3twice = const.tile([P, 2, 2, O], BF16)
        b3cols = const.tile([P, 2, 8], F32)
        neg_raw = const.tile([P, M], F32)
        edge = const.tile([P, M], F32)
        mean_bias = const.tile([P, 1], F32)
        root_bias = const.tile([P, 1], F32)
        shift = const.tile([P, 1], F32)
        zeros = const.tile([P, CH], BF16)

        w2c = keep.tile([P, M, H], U32, align_bytes=256)
        w2s = keep.tile([P, M, H], U8, align_bytes=256)
        w3c = keep.tile([P, M, WP], U32, align_bytes=256)
        w3s = keep.tile([P, M, WP], U8, align_bytes=256)
        q = keep.tile([P, NP, CH], F32)
        acc = keep.tile([P, NP, CH], F32)
        lnq = keep.tile([P, NP, CH], F32)
        spread = keep.tile([P, NP, CH], F32)
        msq = keep.tile([P, NP, CH], F32)
        mean_p = keep.tile([P, NP, CH], F32)
        var_p = keep.tile([P, NP, CH], F32)

        unit = {}
        wt = {}
        pair = {k: {} for k in range(NK)}
        group = {}

        def valid(u):
            return 0 <= u < NU

        def place(u):
            return ROUNDS[u // 2] + (u % 2,)

        def idle_plain(n):
            scratch = psum.tile([P, CH], F32, tag="head", bufs=1, name="scratch")
            for j in range(n):
                nc.tensor.matmul(out=scratch[:], lhsT=zeros[:, 0:P], rhs=zeros[:], start=True, stop=True)

        def setup():
            nc.vector.memset(b3rows[:].rearrange("p s o -> p (s o)"), 0.0)
            nc.scalar.dma_start(out=b3rows[0:M].rearrange("m s o -> m (s o)"), in_=b3)
            nc.scalar.dma_start(out=b2raw[:], in_=b2.rearrange("m (p t) -> p m t", t=4))
            nc.vector.memset(zeros[:], 0.0)
            idle_plain(4)
            make_identity(nc, ident[:])
            nc.vector.tensor_copy(out=ident16[:], in_=ident[:])
            nc.vector.memset(ones[:], 1.0)
            nc.vector.memset(w3c[:], 0)
            nc.vector.memset(w3s[:].rearrange("p m w -> p (m w)").bitcast(U32), 0)
            nc.scalar.activation(out=table_warm[:], in_=ones[:], func=ACT.Sigmoid)

        def bias2():
            nc.vector.tensor_copy(out=b2f[:], in_=b2raw[:])

        def bias3_twice():
            nc.vector.tensor_copy(out=identb[:, 0:M], in_=ident[:, 0:M])
            nc.vector.memset(identb[:, M:8], 1.0)
            nc.vector.tensor_copy(out=b3twice[:], in_=b3rows[:].unsqueeze(2).to_broadcast([P, 2, 2, O]))

        def bias3_turn():
            turned = psum.tile([P, 2, 8], F32, tag="head", bufs=1, name="turned")
            for s in range(2):
                nc.tensor.matmul(
                    out=turned[:, s, :], lhsT=b3twice[:, s].rearrange("p d o -> p (d o)"), rhs=identb[:],
                    start=True, stop=True,
                )
            group["turned"] = turned

        def bias3():
            nc.vector.tensor_copy(out=b3cols[:], in_=group["turned"][:])
            means, raws = b3cols[:, 0, :], b3cols[:, 1, :]
            nc.gpsimd.tensor_scalar(
                out=neg_raw[:], in0=raws[:, 0:M], scalar1=-1.0, scalar2=0.0, op0=ALU.mult, op1=ALU.add
            )
            nc.gpsimd.tensor_scalar(
                out=edge[:], in0=raws[:, 0:M], scalar1=-1.0, scalar2=CLAMP, op0=ALU.mult, op1=ALU.add
            )
            nc.gpsimd.tensor_scalar(
                out=mean_bias[:], in0=means[:, M : M + 1], scalar1=1.0 / M, scalar2=0.0, op0=ALU.mult, op1=ALU.add
            )
            nc.gpsimd.tensor_scalar(
                out=root_bias[:], in0=means[:, M : M + 1], scalar1=1.0 / math.sqrt(M), scalar2=0.0, op0=ALU.mult, op1=ALU.add
            )
            nc.gpsimd.tensor_scalar(
                out=shift[:], in0=raws[:, M : M + 1], scalar1=1.0,
                scalar2=math.log(LN_SCALE) + M * (2 * EPS - CLAMP), op0=ALU.mult, op1=ALU.add,
            )

        def load_w2(m, j=None):
            d = wt.setdefault(m, {})
            if "w2raw" not in d:
                d["w2raw"] = wraw.tile([P, 4 * H], BF16, tag="w2raw", name="w2raw")
            cols = slice(0, 4 * H) if j is None else slice(2 * j * H, 2 * (j + 1) * H)
            nc.sync.dma_start(out=d["w2raw"][:, cols], in_=W2[m].rearrange("(p t) k -> p (t k)", t=4)[:, cols])

        def load_w3(m):
            w3raw = wraw.tile([P, H], BF16, tag="w3raw")
            nc.sync.dma_start(out=w3raw[:], in_=W3[m])
            wt.setdefault(m, {})["w3raw"] = w3raw

        def load_x(u, pieces=1):
            if not valid(u):
                return
            pr, m, h = place(u)
            c = 2 * pr + h
            x = xin.tile([P, R * H], BF16, tag="x")
            n = R * H // pieces
            for j in range(pieces):
                nc.sync.dma_start(
                    out=x[:, j * n : (j + 1) * n],
                    in_=h1[m, c * CH : (c + 1) * CH, :].rearrange("(p r) k -> p (r k)", r=R)[:, j * n : (j + 1) * n],
                )
            unit[u] = {"x": x}

        def transpose_pair(src_words, j):
            bank = psum.tile([P, 2, 2, P], F32, tag="bank")
            for a in range(2):
                for w in range(2):
                    off = (2 * j + a) * 256
                    nc.tensor.transpose(bank[:, a, w, :], src_words[:, off + w : off + 256 : 2], ident[:])
            return bank

        def words_out(copy, grouped, j, bank):
            dst = grouped[:].bitcast(F32).rearrange("q (r c w) -> q r c w", c=P, w=2)
            copy(out=dst[:, 2 * j : 2 * j + 2], in_=bank[:].rearrange("q a w c -> q a c w"))

        def w2_transposes(m, j):
            d = wt[m]
            if m > MATMUL_TURNED:
                d["tp%d" % j] = transpose_pair(d["w2raw"][:].bitcast(F32), j)
                return
            bank = psum.tile([P, 2, 4, P], BF16, tag="bank", name="turned_w2")
            for a in range(2):
                for t in range(4):
                    first = (2 * j + a) * H + t
                    nc.tensor.matmul(
                        out=bank[:, a, t, :], lhsT=d["w2raw"][:, first : first + H - 3 : 4], rhs=ident16[:],
                        start=True, stop=True,
                    )
            d["tp%d" % j] = bank

        def w2_exit(m, j, copy):
            d = wt[m]
            if "gw2" not in d:
                d["gw2"] = work.tile([P, 4 * H], BF16, align_bytes=64, tag="gw2", bufs=2, name="gw2")
            if m > MATMUL_TURNED:
                words_out(copy, d["gw2"], j, d["tp%d" % j])
                return
            dst = d["gw2"][:].rearrange("q (r c t) -> q r c t", c=P, t=4)
            copy(out=dst[:, 2 * j : 2 * j + 2], in_=d["tp%d" % j][:].rearrange("q a t c -> q a c t"))

        def w2_quantise(m, j=None):
            cols = slice(0, H) if j is None else slice(2 * j * P, 2 * (j + 1) * P)
            raw = slice(4 * cols.start, 4 * cols.stop)
            nc.vector.quantize_mx(
                out=w2c[:, m, cols].bitcast(FP8X4), scales=w2s[:, m, cols], in_=wt[m]["gw2"][:, raw]
            )

        def w3_transposes(m):
            d = wt[m]
            w3w = d["w3raw"][:].bitcast(F32).rearrange("o (p w) -> o p w", w=2)
            bank = psum.tile([P, 2, P], F32, tag="bank")
            for w in range(2):
                nc.tensor.transpose(bank[:, w, :], w3w[:, :, w], ident[:])
            d["tp2"] = bank

        def w3_exit(m):
            d = wt[m]
            gw3 = work.tile([P, 4 * O2], BF16, align_bytes=64, tag="gw3", bufs=2)
            nc.vector.tensor_copy(
                out=gw3[:].bitcast(F32).rearrange("p (o w) -> p o w", w=2),
                in_=d["tp2"][:].rearrange("p w o -> p o w"),
            )
            d["gw3"] = gw3

        def w3_quantise(m):
            for s in range(2):
                cols = slice((2 * s + 1) * O, (2 * s + 2) * O)
                nc.vector.quantize_mx(
                    out=w3c[:, m, cols].bitcast(FP8X4),
                    scales=w3s[:, m, cols],
                    in_=wt[m]["gw3"][:, s * 4 * O : (s + 1) * 4 * O],
                )

        def x_transposes(u):
            if valid(u):
                for j in range(2):
                    unit[u]["tp%d" % j] = transpose_pair(unit[u]["x"][:].bitcast(F32), j)

        def x_exit(u, j, copy):
            if not valid(u):
                return
            d = unit[u]
            if j == 0:
                d["g1"] = work.tile([P, 4 * CH], BF16, align_bytes=64, tag="g1", name="g1")
            words_out(copy, d["g1"], j, d["tp%d" % j])

        def quantise1(u):
            if not valid(u):
                return
            d = unit[u]
            c1 = codes.tile([P, CH], U32, align_bytes=256, tag="c1")
            s1 = codes.tile([P, CH], U8, align_bytes=256, tag="s1")
            nc.vector.quantize_mx(out=c1[:].bitcast(FP8X4), scales=s1[:], in_=d["g1"][:])
            d["c1"] = c1
            d["s1"] = s1

        def layer1(u, t):
            if not valid(u):
                return
            d = unit[u]
            m = place(u)[1]
            acc1 = psum.tile([P, CH], F32, tag="bank")
            nc.tensor.matmul_mx(
                out=acc1[:],
                lhsT=w2c[:, m, t * P : (t + 1) * P].bitcast(FP8X4),
                lhsT_scale=w2s[:, m, t * P : (t + 1) * P],
                rhs=d["c1"][:].bitcast(FP8X4),
                rhs_scale=d["s1"][:],
                start=True,
                stop=True,
            )
            d["l1_%d" % t] = acc1

        def h2_exit(u, t, on_vector=False):
            if not valid(u):
                return
            d = unit[u]
            m = place(u)[1]
            if "planes" not in d:
                d["planes"] = work.tile([P, 4, CH], BF16, align_bytes=64, tag="planes", name="planes")
            if on_vector:
                nc.vector.tensor_scalar(
                    out=d["planes"][:, t, :], in0=d["l1_%d" % t][:], scalar1=b2f[:, m, t : t + 1], scalar2=0.0,
                    op0=ALU.add, op1=ALU.max,
                )
            else:
                nc.scalar.activation(
                    out=d["planes"][:, t, :], in_=d["l1_%d" % t][:], func=ACT.Relu, bias=b2f[:, m, t : t + 1], scale=1.0
                )

        def regroup(u):
            if not valid(u):
                return
            d = unit[u]
            g2 = work.tile([P, 4 * CH], BF16, align_bytes=64, tag="g2")
            nc.vector.tensor_copy(
                out=g2[:].rearrange("p (c i t) -> p c t i", i=8, t=4),
                in_=d["planes"][:].rearrange("p t (c i) -> p c t i", i=8),
            )
            d["g2"] = g2

        def quantise2(u):
            if not valid(u):
                return
            d = unit[u]
            c2 = codes.tile([P, CH], U32, align_bytes=256, tag="c2", bufs=NU)
            s2 = codes.tile([P, CH], U8, align_bytes=256, tag="s2", bufs=NU)
            nc.vector.quantize_mx(out=c2[:].bitcast(FP8X4), scales=s2[:], in_=d["g2"][:])
            d["c2"] = c2
            d["s2"] = s2

        def layer2(out, u, side, start, stop):
            d = unit[u]
            pr, m, h = place(u)
            first = 2 * side * O + (1 - h) * O
            nc.tensor.matmul_mx(
                out=out,
                lhsT=w3c[:, m, first : first + P].bitcast(FP8X4),
                lhsT_scale=w3s[:, m, first : first + P],
                rhs=d["c2"][:].bitcast(FP8X4),
                rhs_scale=d["s2"][:],
                start=start,
                stop=stop,
            )

        def head_bank(k, side, tag, bufs):
            pair[k][side] = psum.tile([P, CH], F32, tag=tag, bufs=bufs, name="head_bank")

        def head_pass(k, side, h):
            layer2(pair[k][side][:], 2 * k + h, side, h == 0, h == 1)

        def head_passes(k, side):
            if 0 <= k < NK:
                head_bank(k, side, "head", 1)
                for h in range(2):
                    head_pass(k, side, h)

        def mean_pass(k, h):
            if not 0 <= k < NK:
                return
            pr, m = ROUNDS[k]
            if m == 0 and h == 0:
                tag, bufs = ("mean", 1) if pr == 0 else ("bank", 6)
                group[pr] = psum.tile([P, CH], F32, tag=tag, bufs=bufs, name="mean_sum")
            layer2(group[pr][:], 2 * k + h, 0, m == 0 and h == 0, m == M - 1 and h == 1)

        def mean_passes(*ks):
            for k in ks:
                for h in range(2):
                    mean_pass(k, h)

        def square_means(k):
            if not 0 <= k < NK:
                return
            pr, m = ROUNDS[k]
            tag, bufs = ("sq", 2) if m < KEPT_FROM else ("kept_sq", NP * (M - KEPT_FROM))
            sq = epi.tile([P, CH], F32, tag=tag, bufs=bufs, name="sq")
            nc.scalar.activation(out=sq[:], in_=pair[k][0][:], func=ACT.Square, bias=b3cols[:, 0, m : m + 1], scale=1.0)
            pair[k]["sq"] = sq

        def add_squares(k):
            if not 0 <= k < NK:
                return
            pr, m = ROUNDS[k]
            if 0 < m < KEPT_FROM:
                nc.vector.tensor_tensor(out=acc[:, pr, :], in0=pair[k]["sq"][:], in1=acc[:, pr, :], op=ALU.add)

        def sigmoid_raw(k):
            if not 0 <= k < NK:
                return
            pr, m = ROUNDS[k]
            sg = epi.tile([P, CH], F32, tag="sg")
            nc.scalar.activation(out=sg[:], in_=pair[k][1][:], func=ACT.Sigmoid, bias=neg_raw[:, m : m + 1], scale=-1.0)
            pair[k]["sg"] = sg

        def add_excess(k):
            if not 0 <= k < NK:
                return
            pr, m = ROUNDS[k]
            other = pair[k]["sq"][:] if m == 0 else acc[:, pr, :]
            nc.vector.scalar_tensor_tensor(
                out=acc[:, pr, :], in0=pair[k][1][:], scalar=edge[:, m : m + 1], in1=other, op0=ALU.max, op1=ALU.add
            )

        def multiply_sigmoid(k):
            if not 0 <= k < NK:
                return
            pr, m = ROUNDS[k]
            if m == 0:
                nc.vector.tensor_scalar_max(out=q[:, pr, :], in0=pair[k]["sg"][:], scalar1=DELTA)
            else:
                nc.vector.scalar_tensor_tensor(
                    out=q[:, pr, :], in0=pair[k]["sg"][:], scalar=DELTA, in1=q[:, pr, :], op0=ALU.max, op1=ALU.mult
                )

        def mean_of(pr):
            nc.scalar.activation(
                out=mean_p[:, pr, :], in_=group[pr][:], func=ACT.Identity, bias=mean_bias[:], scale=1.0 / M
            )

        def mean_square(pr):
            nc.scalar.activation(
                out=msq[:, pr, :], in_=group[pr][:], func=ACT.Square, bias=root_bias[:], scale=1.0 / math.sqrt(M)
            )

        def mean_on_vector(pr):
            nc.vector.tensor_scalar(
                out=mean_p[:, pr, :], in0=group[pr][:], scalar1=1.0 / M, scalar2=mean_bias[:, 0:1], op0=ALU.mult, op1=ALU.add
            )

        def square_on_vector(pr):
            nc.vector.scalar_tensor_tensor(
                out=msq[:, pr, :], in0=mean_p[:, pr, :], scalar=float(M), in1=mean_p[:, pr, :], op0=ALU.mult, op1=ALU.mult
            )

        def spread_of(pr):
            nc.vector.scalar_tensor_tensor(
                out=spread[:, pr, :], in0=acc[:, pr, :], scalar=shift[:, 0:1], in1=msq[:, pr, :], op0=ALU.add, op1=ALU.subtract
            )

        def turn_bank(tag="bank", bufs=6):
            return psum.tile([P, R, P], F32, tag=tag, bufs=bufs, name="turned_bank")

        def turn_into(bank, part, first=True, final=True):
            for r in range(R):
                nc.tensor.matmul(
                    out=bank[:, r, :], lhsT=part[:, r * P : (r + 1) * P], rhs=ident[:], is_transpose=True,
                    start=first and r == 0, stop=final and r == R - 1,
                )

        def turn(part, tag="bank", bufs=6):
            bank = turn_bank(tag, bufs)
            turn_into(bank, part)
            return bank

        def turn_squares(bank, ks, first):
            for k in ks:
                turn_into(bank, pair[k]["sq"], first and k == ks[0], False)

        def log_of(pr):
            bank = turn(q[:, pr, :])
            nc.scalar.activation(
                out=lnq[:, pr, :], in_=bank[:].rearrange("p r c -> p (r c)"), func=ACT.Ln, scale=LN_SCALE
            )

        def variance_of(pr, bank):
            nc.vector.tensor_tensor(
                out=var_p[:, pr, :], in0=bank[:].rearrange("p r c -> p (r c)"), in1=lnq[:, pr, :], op=ALU.subtract
            )

        def store(out, pr, fill):
            result = epi.tile([P, 2, R, O], F32, tag="result", bufs=4)
            fill(result)
            nc.sync.dma_start(
                out=out[pr * 2 * CH : (pr + 1) * 2 * CH, :].rearrange("(h p r) o -> p h (r o)", h=2, r=R),
                in_=result[:].rearrange("p h r o -> p h (r o)"),
            )

        def mean_out(pr):
            bank = turn(mean_p[:, pr, :], "mean" if pr == 0 else "head", 1)
            store(out_0, pr, lambda result: nc.scalar.copy(
                out=result[:], in_=bank[:].rearrange("p r (h o) -> p h r o", h=2)))

        def variance_out(pr):
            store(out_1, pr, lambda result: nc.vector.tensor_scalar(
                out=result[:], in0=var_p[:, pr, :].rearrange("p (r h o) -> p h r o", r=R, h=2),
                scalar1=1.0 / M, scalar2=EPS, op0=ALU.mult, op1=ALU.max))

        on_scalar = nc.scalar.copy
        on_vector = nc.vector.tensor_copy

        setup()
        load_w2(0, 0)
        load_x(0, 2)
        load_w2(0, 1)
        load_x(1)
        load_x(2)
        load_w2(1)
        load_w3(0)
        load_x(3)
        load_w3(1)

        w2_transposes(0, 0)
        w2_exit(0, 0, on_vector)
        x_transposes(0)
        x_exit(0, 0, on_scalar)
        w2_transposes(0, 1)
        w2_quantise(0, 0)
        x_exit(0, 1, on_vector)
        w2_exit(0, 1, on_scalar)
        quantise1(0)
        w2_quantise(0, 1)
        bias2()
        x_transposes(1)
        for t in range(4):
            layer1(0, t)

        own = [[k for k in range(NK) if ROUNDS[k][0] == g] for g in range(NP)]

        for i in range(NU):
            even = i % 2 == 0
            k = (i - 4) // 2 if even else (i - 3) // 2
            shared = i % 2 == 1 or i <= 2
            turns2 = [(n, j) for n in range(1, M) for j in range(2) if FIRST[n] - 3 + j == i]
            exits2 = [(n, j) for n in range(1, M) for j in range(2) if FIRST[n] - 2 + j == i]
            turns3 = [n for n in range(M) if max(1, FIRST[n] - 1) == i]
            exits3 = [n for n in range(M) if max(1, FIRST[n] - 1) + 1 == i]
            load_x(i + 4)
            for n in range(2, M):
                if max(1, FIRST[n] - 6) == i:
                    load_w2(n)
                    load_w3(n)
            head_passes(k, 1 if even else 0)
            if NU - 7 <= i < NU - 2:
                mean_passes(own[0][i - NU + 7])
            if i == NU - 1:
                mean_passes(*own[1][:2])
            x_exit(i + 1, 0, on_scalar)
            x_exit(i + 1, 1, on_vector if i <= 1 else on_scalar)
            for t in range(3 if shared else 4):
                h2_exit(i, t)
                for n, j in exits2:
                    if j == 1 and n % 2 == 1 and t == 0:
                        w2_exit(n, j, on_scalar)
                if t == 1:
                    if even:
                        sigmoid_raw(k)
                    else:
                        square_means(k)
            if i <= 1:
                regroup(i - 1)
                quantise1(i + 1)
            if i == 1:
                bias3()
            for n, j in exits2:
                if j == 0 or n % 2 == 0:
                    w2_exit(n, j, on_vector)
            for n in exits3:
                w3_exit(n)
            if i == NU - 1:
                h2_exit(i, 3, True)
            if i > 1:
                regroup(i - 1)
                quantise1(i + 1)
            for n, j in exits2:
                w2_quantise(n, j)
            if shared and i < NU - 1:
                h2_exit(i, 3, True)
            if i == 0:
                bias3_twice()
            if even:
                add_excess(k)
            else:
                multiply_sigmoid((i - 5) // 2)
            quantise2(i - 1)
            if even:
                add_squares(k)
            for n in exits3:
                w3_quantise(n)
            x_transposes(i + 2)
            for n, j in turns2:
                w2_transposes(n, j)
            for n in turns3:
                w3_transposes(n)
            for t in range(4):
                layer1(i + 1, t)
            if i == 0:
                bias3_turn()
        z = NK - 1
        last = NU - 1
        kept = [own[g][KEPT_FROM:] for g in range(NP)]
        sums = [turn_bank() for g in range(NP)]
        turn_squares(sums[0], kept[0], True)
        head_passes(z - 1, 1)
        mean_passes(*own[1][2:4])
        sigmoid_raw(z - 1)
        mean_of(0)
        mean_square(0)
        head_bank(z, 1, "bank", 6)
        head_bank(z, 0, "bank", 6)
        head_pass(z, 1, 0)
        head_pass(z, 0, 0)
        mean_pass(z, 0)
        regroup(last)
        quantise2(last)
        multiply_sigmoid(z - 1)
        add_excess(z - 1)
        head_pass(z, 1, 1)
        head_pass(z, 0, 1)
        mean_pass(z, 1)
        sigmoid_raw(z)
        square_means(z)
        spread_of(0)
        mean_on_vector(1)
        multiply_sigmoid(z)
        add_excess(z)
        square_on_vector(1)
        spread_of(1)
        log_of(0)
        turn_into(sums[0], spread[:, 0, :], False)
        turn_squares(sums[1], kept[1][:-1], True)
        log_of(1)
        turn_squares(sums[1], kept[1][-1:], False)
        mean_out(0)
        mean_out(1)
        turn_into(sums[1], spread[:, 1, :], False)
        variance_of(0, sums[0])
        variance_out(0)
        variance_of(1, sums[1])
        variance_out(1)
